import numpy as np
import ml_dtypes


def mxq(x, axis, fmt="e4m3"):
    dtype, down = {"e4m3": (ml_dtypes.float8_e4m3fn, 7), "e5m2": (ml_dtypes.float8_e5m2, 14)}[fmt]
    v = np.moveaxis(np.asarray(x, np.float32).astype(ml_dtypes.bfloat16).astype(np.float64), axis, -1)
    blocks = v.reshape(v.shape[:-1] + (-1, 32))
    amax = np.abs(blocks).max(-1, keepdims=True)
    byte = np.maximum(np.where(amax > 0, np.frexp(amax)[1] - 1 + 127, 0) - down, 1)
    scale = np.exp2(byte - 127.0)
    codes = (blocks / scale).astype(np.float32).astype(dtype).astype(np.float64)
    return np.moveaxis((codes * scale).reshape(v.shape), -1, axis)


WIDE = False


def mx_kscale(k):
    if not WIDE:
        return np.ones(k)
    levels = np.array([18, -18])
    if k % 512:
        return np.exp2(np.random.permutation(np.resize(levels, k // 32))).repeat(32)
    a = np.empty((k // 512, 16))
    for p in range(k // 512):
        a[p, :8] = np.random.permutation(np.resize(levels, 8))
        for g in range(8):
            far = levels[np.abs(levels - a[p, g]) >= 10]
            a[p, g + 8] = far[np.random.randint(len(far))]
    return np.exp2(a.ravel()).repeat(32)


BF16 = ml_dtypes.bfloat16


def bf(x):
    return np.asarray(x, np.float32).astype(BF16)


def f64(x):
    return np.asarray(x).astype(np.float64)


B, G, WS, C, NH, LK = 1, 64, 32, 256, 4, 512
N = G * G
NW = WS * WS
NG = G // WS
BW = B * NG * NG
DH = C // NH


def setup_inputs():
    s = mx_kscale(NW)
    u = mx_kscale(LK)
    v = mx_kscale(2 * C)
    st = np.broadcast_to(s.reshape(1, 1, WS, 1, WS), (B, NG, WS, NG, WS)).reshape(B, N, 1)
    x0 = bf(np.random.standard_normal((B, N, C)))
    kv_w0 = bf(np.random.standard_normal((C, 2 * C)) / np.sqrt(C))
    kv_b = bf(np.random.standard_normal(2 * C) * 0.3)
    E_k0 = bf(np.random.standard_normal((NW, LK)) / np.sqrt(NW))
    E_v0 = bf(np.random.standard_normal((NW, LK)) * 2.0 / np.sqrt(NW))
    uj = u.reshape(1, 1, LK, 1)
    vk = v[:C].reshape(1, NH, 1, DH)
    vv = v[C:].reshape(1, NH, 1, DH)
    g0 = bf(np.random.standard_normal((BW, NH, LK, DH)) * np.exp2(np.random.randint(-6, 1, (BW, 1, LK, 1))) * uj * vk)
    g1 = bf(np.random.standard_normal((BW, NH, LK, DH)) * np.exp2(np.random.randint(-6, 1, (BW, 1, LK, 1))) * uj * vv)
    return {"x": bf(f64(x0) * st),
            "kv_w": bf(f64(kv_w0) / v),
            "kv_b": kv_b,
            "E_k": bf(f64(E_k0) / s[:, None] / u),
            "E_v": bf(f64(E_v0) / s[:, None] / u),
            "grad_0": g0,
            "grad_1": g1}


def reference(x, kv_w, kv_b, E_k, E_v, grad_0, grad_1):
    g = np.stack([f64(grad_0), f64(grad_1)])
    g = g.transpose(0, 3, 1, 2, 4).reshape(2, LK, BW * C)
    E = np.stack([f64(E_k), f64(E_v)])
    d = mxq(E, 2, "e4m3") @ mxq(g, 1, "e5m2")
    dkv = d.reshape(2, NW, BW, C).transpose(2, 1, 0, 3).reshape(BW, NW, 2 * C)
    dkv = dkv.reshape(B, NG, NG, WS, WS, 2 * C).transpose(0, 1, 3, 2, 4, 5).reshape(B * N, 2 * C)
    dx = mxq(dkv, 1, "e5m2") @ mxq(f64(kv_w), 1, "e4m3").T
    xt = f64(x).reshape(B * N, C)
    dkv_w = mxq(xt, 0, "e4m3").T @ mxq(dkv, 0, "e5m2")
    return dx.reshape(B, N, C), dkv_w

@@ -1,0 +1,421 @@
+from contextlib import ExitStack
+
+import concourse.mybir as mybir
+from concourse.masks import make_identity
+
+F32 = mybir.dt.float32
+BF16 = mybir.dt.bfloat16
+U32 = mybir.dt.uint32
+U8 = mybir.dt.uint8
+E4M3 = mybir.dt.float8_e4m3fn_x4
+E5M2 = mybir.dt.float8_e5m2_x4
+
+FLOPS = 2 * 2 * 4 * 1024 * 512 * 256 + 2 * 2 * 4096 * 512 * 256
+
+
+def tile_efficientspatialwindowattention_pa_v_kernel(
+    tc, x, kv_w, kv_b, e_k, e_v, grad_0, grad_1, out_0, out_1
+):
+    nc = tc.nc
+    es = (e_k, e_v)
+    grads = (grad_0, grad_1)
+    x_view = x.rearrange(
+        "o (a h r b q t) c -> a b h o r q (t c)", a=2, h=2, r=16, b=2, q=8, t=4
+    )
+    dx_view = out_0.rearrange(
+        "o (a h r b q t) c -> a b h o r q (t c)", a=2, h=2, r=16, b=2, q=8, t=4
+    )
+
+    with ExitStack() as ctx:
+        keep = ctx.enter_context(tc.tile_pool(name="keep", bufs=1))
+        rot = ctx.enter_context(tc.tile_pool(name="rot", bufs=3))
+        ps1 = ctx.enter_context(tc.psum_pool(name="ps1", bufs=4))
+        pst = ctx.enter_context(tc.psum_pool(name="pst", bufs=2))
+        psd = ctx.enter_context(tc.psum_pool(name="psd", bufs=2))
+
+        ident = keep.tile([128, 128], F32, name="ident")
+        e_raw = {}
+        e_in = {}
+        e_codes = {}
+        e_scales = {}
+        for kv in range(2):
+            for h in range(2):
+                e_raw[kv, h] = keep.tile([128, 4, 512], BF16, name="e_raw_%d%d" % (kv, h), align_bytes=64)
+                e_codes[kv, h] = keep.tile([128, 512], U32, name="e_codes_%d%d" % (kv, h), align_bytes=64)
+                e_scales[kv, h] = keep.tile([128, 512], U8, name="e_scales_%d%d" % (kv, h), align_bytes=64)
+        g_raw = {}
+        g_in = {}
+        g_codes = {}
+        g_scales = {}
+        for kv in range(2):
+            for w in range(4):
+                g_raw[kv, w] = keep.tile([128, 4, 4, 64], BF16, name="g_raw_%d%d" % (kv, w), align_bytes=64)
+            for wp in range(2):
+                g_codes[kv, wp] = keep.tile([128, 512], U32, name="g_codes_%d%d" % (kv, wp), align_bytes=64)
+                g_scales[kv, wp] = keep.tile([128, 512], U8, name="g_scales_%d%d" % (kv, wp), align_bytes=64)
+        x_raw = {}
+        x_in = {}
+        x_codes = {}
+        x_scales = {}
+        t_codes = {}
+        t_scales = {}
+        for n in range(4):
+            x_raw[n] = keep.tile([128, 2, 1024], BF16, name="x_raw_%d" % n, align_bytes=64)
+            x_codes[n] = keep.tile([128, 512], U32, name="x_codes_%d" % n, align_bytes=64)
+            x_scales[n] = keep.tile([128, 512], U8, name="x_scales_%d" % n, align_bytes=64)
+            for w in range(2):
+                t_codes[n, w] = keep.tile([128, 512], U32, name="t_codes_%d%d" % (n, w), align_bytes=64)
+                t_scales[n, w] = keep.tile([128, 512], U8, name="t_scales_%d%d" % (n, w), align_bytes=64)
+        kw_raw = keep.tile([128, 2, 512], BF16, name="kw_raw", align_bytes=64)
+        kw_in = keep.tile([128, 1024], BF16, name="kw_in", align_bytes=64)
+        kw_codes = keep.tile([128, 768], U32, name="kw_codes", align_bytes=64)
+        kw_scales = keep.tile([128, 768], U8, name="kw_scales", align_bytes=64)
+
+        d = {}
+        banks = {}
+        f_in = {}
+        f_codes = {}
+        f_scales = {}
+        t_in = {}
+        dx = {}
+        o1 = {}
+
+        def load_e(kv, h, tp):
+            src = es[kv].rearrange("(h p t) j -> h p t j", h=2, t=4)
+            nc.sync.dma_start(
+                out=e_raw[kv, h][:, 2 * tp : 2 * tp + 2, :], in_=src[h, :, 2 * tp : 2 * tp + 2, :]
+            )
+
+        def load_g(kv, w):
+            src = grads[kv].rearrange("w h (p j) d -> w p h (j d)", j=4)
+            nc.sync.dma_start(out=g_raw[kv, w][:].rearrange("p h j d -> p h (j d)"), in_=src[w])
+
+        def load_x(n, w):
+            nc.sync.dma_start(out=x_raw[n][:, w, :], in_=x_view[n // 2, w, n % 2, 0])
+
+        def load_kw():
+            nc.sync.dma_start(out=kw_raw[:], in_=kv_w.rearrange("(m p) k -> p m k", m=2))
+
+        def copy(eng, out, in_):
+            if eng == "V":
+                nc.vector.tensor_copy(out=out, in_=in_)
+            else:
+                nc.scalar.copy(out=out, in_=in_)
+
+        def tr_e(kv, h, tp, pool):
+            bank = pool.tile([128, 512], F32, name="bank_e", tag="b")
+            banks["e", kv, h, tp] = bank
+            for t in range(2):
+                words = e_raw[kv, h][:, 2 * tp + t, :].bitcast(F32)
+                for u in range(2):
+                    c0 = (2 * t + u) * 128
+                    nc.tensor.transpose(bank[:, c0 : c0 + 128], words[:, u::2], ident[:])
+
+        def ev_e(eng, kv, h, tp):
+            if tp == 0:
+                e_in[kv, h] = rot.tile([128, 2048], BF16, name="e_in", bufs=2, align_bytes=64)
+            bank = banks["e", kv, h, tp]
+            dst = e_in[kv, h][:].bitcast(F32)[:, tp * 512 : (tp + 1) * 512]
+            copy(
+                eng,
+                dst.rearrange("p (t r u) -> p t r u", t=2, u=2),
+                bank[:].rearrange("p (t u r) -> p t r u", t=2, u=2),
+            )
+
+        def q_e(kv, h):
+            nc.vector.quantize_mx(
+                out=e_codes[kv, h][:].bitcast(E4M3), scales=e_scales[kv, h][:], in_=e_in[kv, h][:]
+            )
+
+        def il_g(kv, w):
+            if w % 2 == 0:
+                g_in[kv, w // 2] = rot.tile([128, 2, 1024], BF16, name="g_in", bufs=2, align_bytes=64)
+            nc.vector.tensor_copy(
+                out=g_in[kv, w // 2][:, w % 2, :].rearrange("p (h d i j) -> p h d j i", h=4, i=4, j=4),
+                in_=g_raw[kv, w][:].rearrange("p h j (d i) -> p h d j i", i=4),
+            )
+
+        def q_g(kv, wp):
+            nc.vector.quantize_mx(
+                out=g_codes[kv, wp][:].bitcast(E5M2),
+                scales=g_scales[kv, wp][:],
+                in_=g_in[kv, wp][:].rearrange("p w f -> p (w f)"),
+            )
+
+        def tr_kw():
+            bank = psd.tile([128, 512], F32, name="bank_kw", tag="b")
+            banks["kw"] = bank
+            for m in range(2):
+                words = kw_raw[:, m, :].bitcast(F32)
+                for u in range(2):
+                    c0 = (2 * m + u) * 128
+                    nc.tensor.transpose(bank[:, c0 : c0 + 128], words[:, u::2], ident[:])
+
+        def ev_kw(eng):
+            copy(
+                eng,
+                kw_in[:].bitcast(F32).rearrange("p (m r u) -> p m r u", m=2, u=2),
+                banks["kw"][:].rearrange("p (m u r) -> p m r u", m=2, u=2),
+            )
+
+        def q_kw():
+            nc.vector.quantize_mx(
+                out=kw_codes[:, 256:512].bitcast(E4M3), scales=kw_scales[:, 256:512], in_=kw_in[:]
+            )
+
+        def il_x(n):
+            x_in[n] = rot.tile([128, 2048], BF16, name="x_in", bufs=2, align_bytes=64)
+            nc.vector.tensor_copy(
+                out=x_in[n][:].rearrange("p (w c i t) -> p w c t i", w=2, i=4, t=4),
+                in_=x_raw[n][:].rearrange("p w (t c i) -> p w c t i", i=4, t=4),
+            )
+
+        def q_x(n):
+            nc.vector.quantize_mx(
+                out=x_codes[n][:].bitcast(E4M3), scales=x_scales[n][:], in_=x_in[n][:]
+            )
+
+        def mm_s1(n, kv, t):
+            if n not in d:
+                d[n] = rot.tile([128, 2, 4, 512], BF16, name="d", bufs=3, align_bytes=64)
+            h = n % 2
+            bank = ps1.tile([128, 512], F32, name="bank_s1", tag="b")
+            banks["s1", n, kv, t] = bank
+            cols = slice(128 * t, 128 * t + 128)
+            nc.tensor.matmul_mx(
+                out=bank[:],
+                lhsT=e_codes[kv, h][:, cols].bitcast(E4M3),
+                lhsT_scale=e_scales[kv, h][:, cols],
+                rhs=g_codes[kv, n // 2][:].bitcast(E5M2),
+                rhs_scale=g_scales[kv, n // 2][:],
+                start=True,
+                stop=True,
+            )
+
+        def ev_s1(eng, n, kv, t):
+            dst = d[n][:, :, t, :].rearrange("p w (u f) -> p w u f", u=2)[:, :, :, 128 * kv : 128 * kv + 128]
+            copy(
+                eng,
+                dst.rearrange("p w u (i e) -> p w u i e", e=2),
+                banks["s1", n, kv, t][:].rearrange("p (w i u e) -> p w u i e", w=2, u=2, e=2),
+            )
+
+        def tr_d(n, t):
+            bank = pst.tile([128, 512], F32, name="bank_t", tag="b")
+            banks["t", n, t] = bank
+            for w in range(2):
+                words = d[n][:, w, t, :].bitcast(F32)
+                for u in range(2):
+                    c0 = (2 * w + u) * 128
+                    nc.tensor.transpose(
+                        bank[:, c0 : c0 + 128], words[:, 128 * u : 128 * u + 128], ident[:]
+                    )
+
+        def ev_t(eng, n, t):
+            if (n, t // 2) not in f_in:
+                f_in[n, t // 2] = rot.tile([128, 2048], BF16, name="f_in", align_bytes=64)
+            dst = f_in[n, t // 2][:].bitcast(F32)[:, (t % 2) * 512 : (t % 2) * 512 + 512]
+            copy(
+                eng,
+                dst.rearrange("p (w r u) -> p w r u", w=2, u=2),
+                banks["t", n, t][:].rearrange("p (w u r) -> p w r u", w=2, u=2),
+            )
+
+        def q_f(n, tp):
+            f_codes[n, tp] = rot.tile([128, 512], U32, name="f_codes", bufs=4, align_bytes=64)
+            f_scales[n, tp] = rot.tile([128, 512], U8, name="f_scales", bufs=4, align_bytes=64)
+            nc.vector.quantize_mx(
+                out=f_codes[n, tp][:].bitcast(E5M2), scales=f_scales[n, tp][:], in_=f_in[n, tp][:]
+            )
+
+        def mm_dx(n, tp, w):
+            bank = psd.tile([128, 512], F32, name="bank_dx", tag="b")
+            banks["dx", n, tp, w] = bank
+            for t in range(2):
+                cols = slice((2 * t + w) * 128, (2 * t + w) * 128 + 128)
+                win = slice(256, 768) if t == 0 else slice(0, 512)
+                nc.tensor.matmul_mx(
+                    out=bank[:],
+                    lhsT=f_codes[n, tp][:, cols].bitcast(E5M2),
+                    lhsT_scale=f_scales[n, tp][:, cols],
+                    rhs=kw_codes[:, win].bitcast(E4M3),
+                    rhs_scale=kw_scales[:, win],
+                    start=(t == 0),
+                    stop=(t == 1),
+                )
+
+        def ev_dx(eng, n, tp, w):
+            if (n, w) not in dx:
+                dx[n, w] = rot.tile([128, 1024], F32, name="dx", bufs=4, align_bytes=64)
+            copy(eng, dx[n, w][:, tp * 512 : tp * 512 + 512], banks["dx", n, tp, w][:])
+
+        def store_dx(n, w, tp=None):
+            rows = slice(0, 1024) if tp is None else slice(512 * tp, 512 * tp + 512)
+            nc.sync.dma_start(
+                out=dx_view[n // 2, w, n % 2, 0][:, :, rows], in_=dx[n, w][:, rows]
+            )
+
+        def il_t(n, w):
+            t_in[n, w] = rot.tile([128, 2048], BF16, name="t_in", bufs=3, align_bytes=64)
+            nc.vector.tensor_copy(
+                out=t_in[n, w][:].rearrange("p (c i t) -> p c t i", i=4, t=4),
+                in_=d[n][:, w, :, :].rearrange("p t (c i) -> p c t i", i=4),
+            )
+
+        def q_t(n, w):
+            nc.vector.quantize_mx(
+                out=t_codes[n, w][:].bitcast(E5M2), scales=t_scales[n, w][:], in_=t_in[n, w][:]
+            )
+
+        def mm_o1(n, w):
+            for m in range(2):
+                if m not in o1:
+                    bank = ps1.tile([128, 512], F32, name="bank_o1", tag="b")
+                    o1[m] = bank
+                cols = slice(256 * w + 128 * m, 256 * w + 128 * m + 128)
+                nc.tensor.matmul_mx(
+                    out=o1[m][:],
+                    lhsT=x_codes[n][:, cols].bitcast(E4M3),
+                    lhsT_scale=x_scales[n][:, cols],
+                    rhs=t_codes[n, w][:].bitcast(E5M2),
+                    rhs_scale=t_scales[n, w][:],
+                    start=(n == 0 and w == 0),
+                    stop=(n == 3 and w == 1),
+                )
+
+        def ev_o1(eng, m):
+            res = keep.tile([128, 512], F32, name="res_%d" % m, align_bytes=64)
+            copy(
+                eng,
+                res[:].rearrange("p (i u e) -> p i u e", u=2, e=2),
+                o1[m][:].rearrange("p (u i e) -> p i u e", u=2, e=2),
+            )
+            nc.sync.dma_start(out=out_1[128 * m : 128 * m + 128, :], in_=res[:])
+
+
+        with tc.manual_schedule():
+            make_identity(nc, ident[:])
+            nc.gpsimd.memset(kw_codes[:, 0:256], 0)
+            nc.gpsimd.memset(kw_codes[:, 512:768], 0)
+            nc.gpsimd.memset(kw_scales[:].bitcast(U32)[:, 0:64], 0)
+            nc.gpsimd.memset(kw_scales[:].bitcast(U32)[:, 128:192], 0)
+            load_e(0, 0, 0)
+            load_g(0, 0)
+            load_g(0, 1)
+            load_e(0, 0, 1)
+            load_e(1, 0, 0)
+            load_e(1, 0, 1)
+            load_g(1, 0)
+            load_g(1, 1)
+            load_x(0, 0)
+            load_x(0, 1)
+            load_e(0, 1, 0)
+            load_e(0, 1, 1)
+            load_g(0, 2)
+            load_g(0, 3)
+            load_e(1, 1, 0)
+            load_e(1, 1, 1)
+            load_kw()
+            load_g(1, 2)
+            load_g(1, 3)
+            for n in range(1, 4):
+                for w in range(2):
+                    load_x(n, w)
+
+            tr_e(0, 0, 0, pst)
+            ev_e("S", 0, 0, 0)
+            il_g(0, 0)
+            il_g(0, 1)
+            tr_e(0, 0, 1, pst)
+            ev_e("S", 0, 0, 1)
+            tr_e(1, 0, 0, psd)
+            tr_e(1, 0, 1, psd)
+            ev_e("S", 1, 0, 0)
+            ev_e("S", 1, 0, 1)
+            q_g(0, 0)
+            q_e(0, 0)
+            for t in range(4):
+                mm_s1(0, 0, t)
+                ev_s1("S", 0, 0, t)
+            il_g(1, 0)
+            il_g(1, 1)
+            q_e(1, 0)
+            q_g(1, 0)
+            il_x(0)
+            for t in range(4):
+                mm_s1(0, 1, t)
+            tr_e(0, 1, 0, psd)
+            tr_e(0, 1, 1, psd)
+            ev_s1("S", 0, 1, 0)
+            ev_s1("S", 0, 1, 1)
+            ev_e("S", 0, 1, 0)
+            ev_e("S", 0, 1, 1)
+            tr_d(0, 0)
+            tr_d(0, 1)
+            tr_e(1, 1, 0, psd)
+            tr_e(1, 1, 1, psd)
+            ev_s1("S", 0, 1, 2)
+            ev_s1("S", 0, 1, 3)
+            ev_e("S", 1, 1, 0)
+            ev_e("S", 1, 1, 1)
+            il_g(0, 2)
+            q_x(0)
+            il_g(0, 3)
+            q_e(0, 1)
+            ev_t("S", 0, 0)
+            ev_t("S", 0, 1)
+            il_t(0, 0)
+            q_e(1, 1)
+            q_g(0, 1)
+            tr_kw()
+            ev_kw("V")
+            q_f(0, 0)
+            q_kw()
+            for i in range(2, 11):
+                n, tp = divmod(i, 2)
+                m, mp = divmod(i - 1, 2)
+                l, lp = divmod(i - 3, 2)
+                if i < 8:
+                    s1 = [(n, kv, t) for t in (2 * tp, 2 * tp + 1) for kv in range(2)]
+                else:
+                    s1 = []
+                for a in s1:
+                    mm_s1(*a)
+                if i > 7:
+                    mm_o1(i - 8, 0)
+                    mm_o1(i - 8, 1)
+                for a in (s1[3:] + s1[:3] if i > 3 else s1):
+                    ev_s1("S", *a)
+                if i < 9:
+                    tr_d(m, 2 * mp)
+                    tr_d(m, 2 * mp + 1)
+                    ev_t("S", m, 2 * mp + 1)
+                    ev_t("S", m, 2 * mp)
+                if i > 2:
+                    mm_dx(l, lp, 0)
+                    mm_dx(l, lp, 1)
+                    ev_dx("S", l, lp, 0)
+                    ev_dx("V" if i in (4, 5, 6) else "S", l, lp, 1)
+                    store_dx(l, 0, lp)
+                    store_dx(l, 1, lp)
+                if 2 < i < 10:
+                    il_t((i - 2) // 2, i % 2)
+                if i == 2:
+                    il_g(1, 2)
+                    il_g(1, 3)
+                if i < 9:
+                    q_f(m, mp)
+                if 3 < i < 11:
+                    q_t((i - 3) // 2, (i - 3) % 2)
+                if i == 2:
+                    q_g(1, 1)
+                if i == 3:
+                    q_t(0, 0)
+                if i in [2,3,5]:
+                    il_x([2,3,5].index(i) + 1)
+                if i in [3,4,6]:
+                    q_x([3,4,6].index(i) + 1)
+            mm_o1(3, 0)
+            mm_o1(3, 1)
+            ev_o1("S", 0)
+            ev_o1("V", 1)

@@ -12,6 +12,8 @@ E5M2 = mybir.dt.float8_e5m2_x4
 
 FLOPS = 2 * 2 * 4 * 1024 * 512 * 256 + 2 * 2 * 4096 * 512 * 256
 
+ROTATING_BANKS = 6
+
 
 def tile_efficientspatialwindowattention_pa_v_kernel(
     tc, x, kv_w, kv_b, e_k, e_v, grad_0, grad_1, out_0, out_1
@@ -28,73 +30,61 @@ def tile_efficientspatialwindowattention_pa_v_kernel(
 
     with ExitStack() as ctx:
         keep = ctx.enter_context(tc.tile_pool(name="keep", bufs=1))
-        rot = ctx.enter_context(tc.tile_pool(name="rot", bufs=3))
-        ps1 = ctx.enter_context(tc.psum_pool(name="ps1", bufs=4))
-        pst = ctx.enter_context(tc.psum_pool(name="pst", bufs=2))
-        psd = ctx.enter_context(tc.psum_pool(name="psd", bufs=2))
+        rot = ctx.enter_context(tc.tile_pool(name="rot", bufs=2))
+        psum = ctx.enter_context(tc.psum_pool(name="psum", bufs=1))
 
-        ident = keep.tile([128, 128], F32, name="ident")
-        e_raw = {}
-        e_in = {}
-        e_codes = {}
-        e_scales = {}
+        def kept(width, dtype, name):
+            return keep.tile([128, width], dtype, name=name, align_bytes=64)
+
+        ident = kept(128, F32, "ident")
+        e_raw, e_in, e_codes, e_scales = {}, {}, {}, {}
+        g_raw, g_in, g_codes, g_scales = {}, {}, {}, {}
         for kv in range(2):
             for h in range(2):
-                e_raw[kv, h] = keep.tile([128, 4, 512], BF16, name="e_raw_%d%d" % (kv, h), align_bytes=64)
-                e_codes[kv, h] = keep.tile([128, 512], U32, name="e_codes_%d%d" % (kv, h), align_bytes=64)
-                e_scales[kv, h] = keep.tile([128, 512], U8, name="e_scales_%d%d" % (kv, h), align_bytes=64)
-        g_raw = {}
-        g_in = {}
-        g_codes = {}
-        g_scales = {}
-        for kv in range(2):
-            for w in range(4):
-                g_raw[kv, w] = keep.tile([128, 4, 4, 64], BF16, name="g_raw_%d%d" % (kv, w), align_bytes=64)
-            for wp in range(2):
-                g_codes[kv, wp] = keep.tile([128, 512], U32, name="g_codes_%d%d" % (kv, wp), align_bytes=64)
-                g_scales[kv, wp] = keep.tile([128, 512], U8, name="g_scales_%d%d" % (kv, wp), align_bytes=64)
-        x_raw = {}
-        x_in = {}
-        x_codes = {}
-        x_scales = {}
-        t_codes = {}
-        t_scales = {}
+                for tp in range(2):
+                    e_raw[kv, h, tp] = kept(1024, BF16, "e_raw_%d%d%d" % (kv, h, tp))
+                e_codes[kv, h] = kept(512, U32, "e_codes_%d%d" % (kv, h))
+                e_scales[kv, h] = kept(512, U8, "e_scales_%d%d" % (kv, h))
+            for a in range(2):
+                g_raw[kv, a] = kept(2048, BF16, "g_raw_%d%d" % (kv, a))
+                g_codes[kv, a] = kept(512, U32, "g_codes_%d%d" % (kv, a))
+                g_scales[kv, a] = kept(512, U8, "g_scales_%d%d" % (kv, a))
+        x_raw, x_in, x_codes, x_scales, t_codes, t_scales = {}, {}, {}, {}, {}, {}
         for n in range(4):
-            x_raw[n] = keep.tile([128, 2, 1024], BF16, name="x_raw_%d" % n, align_bytes=64)
-            x_codes[n] = keep.tile([128, 512], U32, name="x_codes_%d" % n, align_bytes=64)
-            x_scales[n] = keep.tile([128, 512], U8, name="x_scales_%d" % n, align_bytes=64)
-            for w in range(2):
-                t_codes[n, w] = keep.tile([128, 512], U32, name="t_codes_%d%d" % (n, w), align_bytes=64)
-                t_scales[n, w] = keep.tile([128, 512], U8, name="t_scales_%d%d" % (n, w), align_bytes=64)
-        kw_raw = keep.tile([128, 2, 512], BF16, name="kw_raw", align_bytes=64)
-        kw_in = keep.tile([128, 1024], BF16, name="kw_in", align_bytes=64)
-        kw_codes = keep.tile([128, 768], U32, name="kw_codes", align_bytes=64)
-        kw_scales = keep.tile([128, 768], U8, name="kw_scales", align_bytes=64)
+            x_raw[n] = kept(2048, BF16, "x_raw_%d" % n)
+            x_codes[n] = kept(512, U32, "x_codes_%d" % n)
+            x_scales[n] = kept(512, U8, "x_scales_%d" % n)
+        kw_raw = kept(1024, BF16, "kw_raw")
+        kw_in = kept(1024, BF16, "kw_in")
+        kw_codes = kept(768, U32, "kw_codes")
+        kw_scales = kept(768, U8, "kw_scales")
 
-        d = {}
-        banks = {}
-        f_in = {}
-        f_codes = {}
-        f_scales = {}
-        t_in = {}
-        dx = {}
-        o1 = {}
+        d, banks, f_in, f_codes, f_scales, t_in, dx, o1 = {}, {}, {}, {}, {}, {}, {}, {}
+        taken = []
+
+        def next_bank(key, tag=None):
+            if tag is None:
+                tag = "bank_%d" % (len(taken) % ROTATING_BANKS)
+                taken.append(key)
+            banks[key] = psum.tile([128, 512], F32, name="bank", tag=tag)
+            return banks[key]
 
         def load_e(kv, h, tp):
-            src = es[kv].rearrange("(h p t) j -> h p t j", h=2, t=4)
-            nc.sync.dma_start(
-                out=e_raw[kv, h][:, 2 * tp : 2 * tp + 2, :], in_=src[h, :, 2 * tp : 2 * tp + 2, :]
-            )
+            src = es[kv].rearrange("(h p tp t) j -> h tp p (t j)", h=2, tp=2, t=2)
+            nc.sync.dma_start(out=e_raw[kv, h, tp][:], in_=src[h, tp])
 
         def load_g(kv, w):
             src = grads[kv].rearrange("w h (p j) d -> w p h (j d)", j=4)
-            nc.sync.dma_start(out=g_raw[kv, w][:].rearrange("p h j d -> p h (j d)"), in_=src[w])
+            dst = g_raw[kv, w // 2][:, 1024 * (w % 2) : 1024 * (w % 2) + 1024]
+            nc.sync.dma_start(out=dst.rearrange("p (h f) -> p h f", h=4), in_=src[w])
 
-        def load_x(n, w):
-            nc.sync.dma_start(out=x_raw[n][:, w, :], in_=x_view[n // 2, w, n % 2, 0])
+        def load_x(n, b):
+            nc.sync.dma_start(out=x_raw[n][:, 1024 * b : 1024 * b + 1024], in_=x_view[n // 2, b, n % 2, 0])
 
         def load_kw():
-            nc.sync.dma_start(out=kw_raw[:], in_=kv_w.rearrange("(m p) k -> p m k", m=2))
+            nc.sync.dma_start(
+                out=kw_raw[:].rearrange("p (m k) -> p m k", m=2), in_=kv_w.rearrange("(m p) k -> p m k", m=2)
+            )
 
         def copy(eng, out, in_):
             if eng == "V":
@@ -102,85 +92,80 @@ def tile_efficientspatialwindowattention_pa_v_kernel(
             else:
                 nc.scalar.copy(out=out, in_=in_)
 
-        def tr_e(kv, h, tp, pool):
-            bank = pool.tile([128, 512], F32, name="bank_e", tag="b")
-            banks["e", kv, h, tp] = bank
+        def transpose_rows(raw, key, tag):
+            bank = next_bank(key, tag)
             for t in range(2):
-                words = e_raw[kv, h][:, 2 * tp + t, :].bitcast(F32)
+                words = raw[:, 512 * t : 512 * t + 512].bitcast(F32)
                 for u in range(2):
                     c0 = (2 * t + u) * 128
                     nc.tensor.transpose(bank[:, c0 : c0 + 128], words[:, u::2], ident[:])
 
-        def ev_e(eng, kv, h, tp):
-            if tp == 0:
-                e_in[kv, h] = rot.tile([128, 2048], BF16, name="e_in", bufs=2, align_bytes=64)
-            bank = banks["e", kv, h, tp]
-            dst = e_in[kv, h][:].bitcast(F32)[:, tp * 512 : (tp + 1) * 512]
+        def join_halves(eng, dst, key):
             copy(
                 eng,
-                dst.rearrange("p (t r u) -> p t r u", t=2, u=2),
-                bank[:].rearrange("p (t u r) -> p t r u", t=2, u=2),
+                dst.bitcast(F32).rearrange("p (t r u) -> p t r u", t=2, u=2),
+                banks[key][:].rearrange("p (t u r) -> p t r u", t=2, u=2),
             )
 
-        def q_e(kv, h):
+        def tr_e(kv, h, tp, tag=None):
+            transpose_rows(e_raw[kv, h, tp], ("e", kv, h, tp), tag)
+
+        def ev_e(eng, kv, h, tp):
+            if (kv, h) not in e_in:
+                e_in[kv, h] = rot.tile([128, 2048], BF16, name="e_in", align_bytes=64)
+            join_halves(eng, e_in[kv, h][:, 1024 * tp : 1024 * tp + 1024], ("e", kv, h, tp))
+
+        def q_e(kv, h, tp=None):
+            lo, hi = (0, 512) if tp is None else (256 * tp, 256 * tp + 256)
             nc.vector.quantize_mx(
-                out=e_codes[kv, h][:].bitcast(E4M3), scales=e_scales[kv, h][:], in_=e_in[kv, h][:]
+                out=e_codes[kv, h][:, lo:hi].bitcast(E4M3),
+                scales=e_scales[kv, h][:, lo:hi],
+                in_=e_in[kv, h][:, 4 * lo : 4 * hi],
             )
 
-        def il_g(kv, w):
-            if w % 2 == 0:
-                g_in[kv, w // 2] = rot.tile([128, 2, 1024], BF16, name="g_in", bufs=2, align_bytes=64)
-            nc.vector.tensor_copy(
-                out=g_in[kv, w // 2][:, w % 2, :].rearrange("p (h d i j) -> p h d j i", h=4, i=4, j=4),
-                in_=g_raw[kv, w][:].rearrange("p h j (d i) -> p h d j i", i=4),
+        def il_g(eng, kv, a, b=None):
+            if (kv, a) not in g_in:
+                g_in[kv, a] = rot.tile([128, 2048], BF16, name="g_in", align_bytes=64)
+            cols = slice(0, 2048) if b is None else slice(1024 * b, 1024 * b + 1024)
+            copy(
+                eng,
+                g_in[kv, a][:, cols].rearrange("p (h d i j) -> p h d j i", d=16, i=4, j=4),
+                g_raw[kv, a][:, cols].rearrange("p (h j d i) -> p h d j i", d=16, j=4, i=4),
             )
 
-        def q_g(kv, wp):
+        def q_g(kv, a, b=None):
+            lo, hi = (0, 512) if b is None else (256 * b, 256 * b + 256)
             nc.vector.quantize_mx(
-                out=g_codes[kv, wp][:].bitcast(E5M2),
-                scales=g_scales[kv, wp][:],
-                in_=g_in[kv, wp][:].rearrange("p w f -> p (w f)"),
+                out=g_codes[kv, a][:, lo:hi].bitcast(E5M2),
+                scales=g_scales[kv, a][:, lo:hi],
+                in_=g_in[kv, a][:, 4 * lo : 4 * hi],
             )
 
-        def tr_kw():
-            bank = psd.tile([128, 512], F32, name="bank_kw", tag="b")
-            banks["kw"] = bank
-            for m in range(2):
-                words = kw_raw[:, m, :].bitcast(F32)
-                for u in range(2):
-                    c0 = (2 * m + u) * 128
-                    nc.tensor.transpose(bank[:, c0 : c0 + 128], words[:, u::2], ident[:])
+        def tr_kw(tag=None):
+            transpose_rows(kw_raw, "kw", tag)
 
         def ev_kw(eng):
-            copy(
-                eng,
-                kw_in[:].bitcast(F32).rearrange("p (m r u) -> p m r u", m=2, u=2),
-                banks["kw"][:].rearrange("p (m u r) -> p m r u", m=2, u=2),
-            )
+            join_halves(eng, kw_in[:], "kw")
 
         def q_kw():
             nc.vector.quantize_mx(
                 out=kw_codes[:, 256:512].bitcast(E4M3), scales=kw_scales[:, 256:512], in_=kw_in[:]
             )
 
-        def il_x(n):
-            x_in[n] = rot.tile([128, 2048], BF16, name="x_in", bufs=2, align_bytes=64)
-            nc.vector.tensor_copy(
-                out=x_in[n][:].rearrange("p (w c i t) -> p w c t i", w=2, i=4, t=4),
-                in_=x_raw[n][:].rearrange("p w (t c i) -> p w c t i", i=4, t=4),
+        def il_x(eng, n):
+            x_in[n] = rot.tile([128, 2048], BF16, name="x_in", align_bytes=64)
+            copy(
+                eng,
+                x_in[n][:].rearrange("p (b c i t) -> p b c t i", b=2, i=4, t=4),
+                x_raw[n][:].rearrange("p (b t c i) -> p b c t i", b=2, i=4, t=4),
             )
 
         def q_x(n):
-            nc.vector.quantize_mx(
-                out=x_codes[n][:].bitcast(E4M3), scales=x_scales[n][:], in_=x_in[n][:]
-            )
+            nc.vector.quantize_mx(out=x_codes[n][:].bitcast(E4M3), scales=x_scales[n][:], in_=x_in[n][:])
 
         def mm_s1(n, kv, t):
-            if n not in d:
-                d[n] = rot.tile([128, 2, 4, 512], BF16, name="d", bufs=3, align_bytes=64)
             h = n % 2
-            bank = ps1.tile([128, 512], F32, name="bank_s1", tag="b")
-            banks["s1", n, kv, t] = bank
+            bank = next_bank(("s1", n, kv, t))
             cols = slice(128 * t, 128 * t + 128)
             nc.tensor.matmul_mx(
                 out=bank[:],
@@ -193,46 +178,34 @@ def tile_efficientspatialwindowattention_pa_v_kernel(
             )
 
         def ev_s1(eng, n, kv, t):
-            dst = d[n][:, :, t, :].rearrange("p w (u f) -> p w u f", u=2)[:, :, :, 128 * kv : 128 * kv + 128]
-            copy(
-                eng,
-                dst.rearrange("p w u (i e) -> p w u i e", e=2),
-                banks["s1", n, kv, t][:].rearrange("p (w i u e) -> p w u i e", w=2, u=2, e=2),
-            )
+            if n not in d:
+                d[n] = rot.tile([128, 4096], BF16, name="d", bufs=4, align_bytes=64)
+            dst = d[n][:].rearrange("p (t b u k i e) -> p t k b u i e", t=4, b=2, u=2, k=2, e=2)[:, t, kv]
+            copy(eng, dst, banks["s1", n, kv, t][:].rearrange("p (b i u e) -> p b u i e", b=2, u=2, e=2))
 
         def tr_d(n, t):
-            bank = pst.tile([128, 512], F32, name="bank_t", tag="b")
-            banks["t", n, t] = bank
-            for w in range(2):
-                words = d[n][:, w, t, :].bitcast(F32)
-                for u in range(2):
-                    c0 = (2 * w + u) * 128
-                    nc.tensor.transpose(
-                        bank[:, c0 : c0 + 128], words[:, 128 * u : 128 * u + 128], ident[:]
-                    )
+            bank = next_bank(("t", n, t))
+            words = d[n][:, 1024 * t : 1024 * t + 1024].bitcast(F32)
+            for s in range(4):
+                cols = slice(128 * s, 128 * s + 128)
+                nc.tensor.transpose(bank[:, cols], words[:, cols], ident[:])
 
         def ev_t(eng, n, t):
             if (n, t // 2) not in f_in:
-                f_in[n, t // 2] = rot.tile([128, 2048], BF16, name="f_in", align_bytes=64)
-            dst = f_in[n, t // 2][:].bitcast(F32)[:, (t % 2) * 512 : (t % 2) * 512 + 512]
-            copy(
-                eng,
-                dst.rearrange("p (w r u) -> p w r u", w=2, u=2),
-                banks["t", n, t][:].rearrange("p (w u r) -> p w r u", w=2, u=2),
-            )
+                f_in[n, t // 2] = rot.tile([128, 2048], BF16, name="f_in", bufs=3, align_bytes=64)
+            join_halves(eng, f_in[n, t // 2][:, 1024 * (t % 2) : 1024 * (t % 2) + 1024], ("t", n, t))
 
         def q_f(n, tp):
-            f_codes[n, tp] = rot.tile([128, 512], U32, name="f_codes", bufs=4, align_bytes=64)
-            f_scales[n, tp] = rot.tile([128, 512], U8, name="f_scales", bufs=4, align_bytes=64)
+            f_codes[n, tp] = rot.tile([128, 512], U32, name="f_codes", bufs=8, align_bytes=64)
+            f_scales[n, tp] = rot.tile([128, 512], U8, name="f_scales", bufs=8, align_bytes=64)
             nc.vector.quantize_mx(
                 out=f_codes[n, tp][:].bitcast(E5M2), scales=f_scales[n, tp][:], in_=f_in[n, tp][:]
             )
 
-        def mm_dx(n, tp, w):
-            bank = psd.tile([128, 512], F32, name="bank_dx", tag="b")
-            banks["dx", n, tp, w] = bank
+        def mm_dx(n, tp, b):
+            bank = next_bank(("dx", n, tp, b))
             for t in range(2):
-                cols = slice((2 * t + w) * 128, (2 * t + w) * 128 + 128)
+                cols = slice((2 * t + b) * 128, (2 * t + b) * 128 + 128)
                 win = slice(256, 768) if t == 0 else slice(0, 512)
                 nc.tensor.matmul_mx(
                     out=bank[:],
@@ -244,47 +217,51 @@ def tile_efficientspatialwindowattention_pa_v_kernel(
                     stop=(t == 1),
                 )
 
-        def ev_dx(eng, n, tp, w):
-            if (n, w) not in dx:
-                dx[n, w] = rot.tile([128, 1024], F32, name="dx", bufs=4, align_bytes=64)
-            copy(eng, dx[n, w][:, tp * 512 : tp * 512 + 512], banks["dx", n, tp, w][:])
-
-        def store_dx(n, w, tp=None):
-            rows = slice(0, 1024) if tp is None else slice(512 * tp, 512 * tp + 512)
+        def ev_dx(eng, n, tp, b):
+            dx[n, tp, b] = rot.tile([128, 512], F32, name="dx", bufs=6, align_bytes=64)
+            copy(eng, dx[n, tp, b][:], banks["dx", n, tp, b][:])
             nc.sync.dma_start(
-                out=dx_view[n // 2, w, n % 2, 0][:, :, rows], in_=dx[n, w][:, rows]
+                out=dx_view[n // 2, b, n % 2, 0][:, :, 512 * tp : 512 * tp + 512], in_=dx[n, tp, b][:]
             )
 
-        def il_t(n, w):
-            t_in[n, w] = rot.tile([128, 2048], BF16, name="t_in", bufs=3, align_bytes=64)
-            nc.vector.tensor_copy(
-                out=t_in[n, w][:].rearrange("p (c i t) -> p c t i", i=4, t=4),
-                in_=d[n][:, w, :, :].rearrange("p t (c i) -> p c t i", i=4),
+        def il_t(eng, n, kv):
+            if n not in t_in:
+                t_in[n] = rot.tile([128, 4096], BF16, name="t_in", align_bytes=64)
+            copy(
+                eng,
+                t_in[n][:].rearrange("p (s k c i t) -> p k s c t i", s=4, k=2, i=4, t=4)[:, kv],
+                d[n][:].rearrange("p (t s k c i) -> p k s c t i", t=4, s=4, k=2, i=4)[:, kv],
             )
 
-        def q_t(n, w):
+        def q_t(n, b=None):
+            if n not in t_codes:
+                t_codes[n] = rot.tile([128, 1024], U32, name="t_codes", bufs=3, align_bytes=64)
+                t_scales[n] = rot.tile([128, 1024], U8, name="t_scales", bufs=3, align_bytes=64)
+            lo, hi = (0, 1024) if b is None else (512 * b, 512 * b + 512)
             nc.vector.quantize_mx(
-                out=t_codes[n, w][:].bitcast(E5M2), scales=t_scales[n, w][:], in_=t_in[n, w][:]
+                out=t_codes[n][:, lo:hi].bitcast(E5M2),
+                scales=t_scales[n][:, lo:hi],
+                in_=t_in[n][:, 4 * lo : 4 * hi],
             )
 
-        def mm_o1(n, w):
+        def mm_o1(n, b):
             for m in range(2):
                 if m not in o1:
-                    bank = ps1.tile([128, 512], F32, name="bank_o1", tag="b")
-                    o1[m] = bank
-                cols = slice(256 * w + 128 * m, 256 * w + 128 * m + 128)
+                    o1[m] = next_bank(("o1", m), "held_%d" % m)
+                cols = slice(256 * b + 128 * m, 256 * b + 128 * m + 128)
+                win = slice(512 * b, 512 * b + 512)
                 nc.tensor.matmul_mx(
                     out=o1[m][:],
                     lhsT=x_codes[n][:, cols].bitcast(E4M3),
                     lhsT_scale=x_scales[n][:, cols],
-                    rhs=t_codes[n, w][:].bitcast(E5M2),
-                    rhs_scale=t_scales[n, w][:],
-                    start=(n == 0 and w == 0),
-                    stop=(n == 3 and w == 1),
+                    rhs=t_codes[n][:, win].bitcast(E5M2),
+                    rhs_scale=t_scales[n][:, win],
+                    start=(n == 0 and b == 0),
+                    stop=(n == 3 and b == 1),
                 )
 
         def ev_o1(eng, m):
-            res = keep.tile([128, 512], F32, name="res_%d" % m, align_bytes=64)
+            res = kept(512, F32, "res_%d" % m)
             copy(
                 eng,
                 res[:].rearrange("p (i u e) -> p i u e", u=2, e=2),
@@ -292,6 +269,94 @@ def tile_efficientspatialwindowattention_pa_v_kernel(
             )
             nc.sync.dma_start(out=out_1[128 * m : 128 * m + 128, :], in_=res[:])
 
+
+        def needs(op):
+            kind, a = op[0], op[1:]
+            if kind == "ev_e":
+                kv, h, tp = a
+                return [("tr_e",) + a] + ([("q_e", 0, h)] if kv else [])
+            if kind == "q_e":
+                return [("ev_e",) + a] if len(a) == 3 else [("ev_e",) + a + (tp,) for tp in range(2)]
+            if kind == "il_g":
+                return [("q_g", a[0], 0)] if a[1] else []
+            if kind == "q_g":
+                return [("il_g",) + a]
+            if kind == "ev_kw":
+                return [("tr_kw",)]
+            if kind == "q_kw":
+                return [("ev_kw",)]
+            if kind == "il_x":
+                return [("q_x", a[0] - 2)] if a[0] > 1 else []
+            if kind == "q_x":
+                return [("il_x",) + a]
+            if kind == "mm_s1":
+                n, kv, t = a
+                return [("q_e", kv, n % 2, t // 2), ("q_g", kv, n // 2)]
+            if kind == "ev_s1":
+                return [("mm_s1",) + a]
+            if kind == "tr_d":
+                n, t = a
+                return [("ev_s1", n, 0, t), ("ev_s1", n, 1, t)]
+            if kind == "ev_t":
+                n, t = a
+                f = 2 * n + t // 2 - 3
+                return [("tr_d",) + a] + ([("q_f", f // 2, f % 2)] if f >= 0 else [])
+            if kind == "q_f":
+                n, tp = a
+                return [("ev_t", n, 2 * tp), ("ev_t", n, 2 * tp + 1)]
+            if kind == "mm_dx":
+                return [("q_f", a[0], a[1]), ("q_kw",)]
+            if kind == "ev_dx":
+                return [("mm_dx",) + a]
+            if kind == "il_t":
+                n, kv = a
+                old = [("q_t", n - 2, b) for b in range(2)] if n > 1 else []
+                return [("ev_s1", n, kv, t) for t in range(4)] + old
+            if kind == "q_t":
+                n = a[0]
+                old = [("mm_o1", n - 3, s) for s in range(2)] if n > 2 else []
+                return [("il_t", n, 0), ("il_t", n, 1)] + old
+            if kind == "mm_o1":
+                return [("q_t",) + a, ("q_x", a[0])]
+            if kind == "ev_o1":
+                return [("mm_o1", 3, 1)]
+            return []
+
+        calls = {
+            "tr_e": tr_e, "ev_e": ev_e, "q_e": q_e, "il_g": il_g, "q_g": q_g, "tr_kw": tr_kw, "ev_kw": ev_kw,
+            "q_kw": q_kw, "il_x": il_x, "q_x": q_x, "mm_s1": mm_s1, "ev_s1": ev_s1, "tr_d": tr_d, "ev_t": ev_t,
+            "q_f": q_f, "mm_dx": mm_dx, "ev_dx": ev_dx, "il_t": il_t, "q_t": q_t, "mm_o1": mm_o1, "ev_o1": ev_o1,
+        }
+        emptied_by = {"tr_e": "ev_e", "tr_kw": "ev_kw", "mm_s1": "ev_s1", "tr_d": "ev_t", "mm_dx": "ev_dx"}
+
+        parts = {"q_e": 4, "il_g": 4, "q_g": 4, "q_t": 3}
+
+        def write_in_order(queues):
+            fills = [op for op in queues["T"] if op[0] in emptied_by]
+            written = set()
+            heads = {eng: 0 for eng in queues}
+            for sweep in range(sum(len(q) for q in queues.values())):
+                for eng in queues:
+                    if heads[eng] == len(queues[eng]):
+                        continue
+                    op = queues[eng][heads[eng]]
+                    wanted = needs(op)
+                    if op in fills and fills.index(op) >= ROTATING_BANKS:
+                        old = fills[fills.index(op) - ROTATING_BANKS]
+                        wanted = wanted + [(emptied_by[old[0]],) + old[1:]]
+                    if all(w in written for w in wanted):
+                        if op[0][:2] in ("ev", "il"):
+                            calls[op[0]](eng, *op[1:])
+                        else:
+                            calls[op[0]](*op[1:])
+                        written.add(op)
+                        if len(op) < parts.get(op[0], 0):
+                            written.add(op + (0,))
+                            written.add(op + (1,))
+                        elif op[0] in parts and op[:-1] + (1 - op[-1],) in written:
+                            written.add(op[:-1])
+                        heads[eng] = heads[eng] + 1
+            assert all(heads[eng] == len(queues[eng]) for eng in queues)
 
         with tc.manual_schedule():
             make_identity(nc, ident[:])
@@ -303,119 +368,61 @@ def tile_efficientspatialwindowattention_pa_v_kernel(
             load_g(0, 0)
             load_g(0, 1)
             load_e(0, 0, 1)
-            load_e(1, 0, 0)
-            load_e(1, 0, 1)
-            load_g(1, 0)
-            load_g(1, 1)
-            load_x(0, 0)
-            load_x(0, 1)
             load_e(0, 1, 0)
             load_e(0, 1, 1)
-            load_g(0, 2)
-            load_g(0, 3)
-            load_e(1, 1, 0)
-            load_e(1, 1, 1)
+            load_g(1, 0)
+            load_g(1, 1)
+            for h in range(2):
+                for tp in range(2):
+                    load_e(1, h, tp)
+            load_x(0, 0)
+            load_x(0, 1)
             load_kw()
-            load_g(1, 2)
-            load_g(1, 3)
+            for kv in range(2):
+                for w in range(2, 4):
+                    load_g(kv, w)
             for n in range(1, 4):
-                for w in range(2):
-                    load_x(n, w)
+                for b in range(2):
+                    load_x(n, b)
 
-            tr_e(0, 0, 0, pst)
-            ev_e("S", 0, 0, 0)
-            il_g(0, 0)
-            il_g(0, 1)
-            tr_e(0, 0, 1, pst)
-            ev_e("S", 0, 0, 1)
-            tr_e(1, 0, 0, psd)
-            tr_e(1, 0, 1, psd)
-            ev_e("S", 1, 0, 0)
-            ev_e("S", 1, 0, 1)
-            q_g(0, 0)
-            q_e(0, 0)
-            for t in range(4):
-                mm_s1(0, 0, t)
-                ev_s1("S", 0, 0, t)
-            il_g(1, 0)
-            il_g(1, 1)
-            q_e(1, 0)
-            q_g(1, 0)
-            il_x(0)
-            for t in range(4):
-                mm_s1(0, 1, t)
-            tr_e(0, 1, 0, psd)
-            tr_e(0, 1, 1, psd)
-            ev_s1("S", 0, 1, 0)
-            ev_s1("S", 0, 1, 1)
-            ev_e("S", 0, 1, 0)
-            ev_e("S", 0, 1, 1)
-            tr_d(0, 0)
-            tr_d(0, 1)
-            tr_e(1, 1, 0, psd)
-            tr_e(1, 1, 1, psd)
-            ev_s1("S", 0, 1, 2)
-            ev_s1("S", 0, 1, 3)
-            ev_e("S", 1, 1, 0)
-            ev_e("S", 1, 1, 1)
-            il_g(0, 2)
-            q_x(0)
-            il_g(0, 3)
-            q_e(0, 1)
-            ev_t("S", 0, 0)
-            ev_t("S", 0, 1)
-            il_t(0, 0)
-            q_e(1, 1)
-            q_g(0, 1)
-            tr_kw()
-            ev_kw("V")
-            q_f(0, 0)
-            q_kw()
-            for i in range(2, 11):
-                n, tp = divmod(i, 2)
-                m, mp = divmod(i - 1, 2)
-                l, lp = divmod(i - 3, 2)
-                if i < 8:
-                    s1 = [(n, kv, t) for t in (2 * tp, 2 * tp + 1) for kv in range(2)]
-                else:
-                    s1 = []
-                for a in s1:
-                    mm_s1(*a)
-                if i > 7:
-                    mm_o1(i - 8, 0)
-                    mm_o1(i - 8, 1)
-                for a in (s1[3:] + s1[:3] if i > 3 else s1):
-                    ev_s1("S", *a)
-                if i < 9:
-                    tr_d(m, 2 * mp)
-                    tr_d(m, 2 * mp + 1)
-                    ev_t("S", m, 2 * mp + 1)
-                    ev_t("S", m, 2 * mp)
-                if i > 2:
-                    mm_dx(l, lp, 0)
-                    mm_dx(l, lp, 1)
-                    ev_dx("S", l, lp, 0)
-                    ev_dx("V" if i in (4, 5, 6) else "S", l, lp, 1)
-                    store_dx(l, 0, lp)
-                    store_dx(l, 1, lp)
-                if 2 < i < 10:
-                    il_t((i - 2) // 2, i % 2)
-                if i == 2:
-                    il_g(1, 2)
-                    il_g(1, 3)
-                if i < 9:
-                    q_f(m, mp)
-                if 3 < i < 11:
-                    q_t((i - 3) // 2, (i - 3) % 2)
-                if i == 2:
-                    q_g(1, 1)
-                if i == 3:
-                    q_t(0, 0)
-                if i in [2,3,5]:
-                    il_x([2,3,5].index(i) + 1)
-                if i in [3,4,6]:
-                    q_x([3,4,6].index(i) + 1)
-            mm_o1(3, 0)
-            mm_o1(3, 1)
-            ev_o1("S", 0)
-            ev_o1("V", 1)
+            def s1(kind, n, kv, ts):
+                return [(kind, n, kv, t) for t in ts]
+
+            def half(kind, f):
+                return [(kind, f // 2, f % 2)]
+
+            def tpair(kind, f, ts):
+                return [(kind, f // 2, 2 * (f % 2) + t) for t in ts]
+
+            def dxs(kind, f, bs):
+                return [(kind, f // 2, f % 2, b) for b in bs]
+
+            def ee(kind, kv, h, tps=(0, 1)):
+                return [(kind, kv, h, tp) for tp in tps]
+
+
+            te = ee("tr_e", 0, 0) + ee("tr_e", 0, 1, (0,)) + s1("mm_s1", 0, 0, (0, 1)) + ee("tr_e", 0, 1, (1,)) + s1("mm_s1", 0, 0, (2, 3))
+            te += ee("tr_e", 1, 0) + s1("mm_s1", 1, 0, (0, 1)) + ee("tr_e", 1, 1) + s1("mm_s1", 1, 0, (2, 3))
+            te += s1("mm_s1", 0, 1, (0, 1)) + [("tr_kw",)] + s1("mm_s1", 0, 1, (2, 3)) + tpair("tr_d", 0, (0, 1))
+            te += s1("mm_s1", 1, 1, (0, 1)) + tpair("tr_d", 1, (0, 1)) + s1("mm_s1", 1, 1, (2, 3)) + tpair("tr_d", 2, (0, 1))
+            sc = ee("ev_e", 0, 0) + ee("ev_e", 0, 1, (0,)) + s1("ev_s1", 0, 0, (0, 1)) + ee("ev_e", 0, 1, (1,)) + s1("ev_s1", 0, 0, (2, 3))
+            sc += ee("ev_e", 1, 0, (0,)) + s1("ev_s1", 1, 0, (1, 0)) + ee("ev_e", 1, 1, (1, 0)) + s1("ev_s1", 1, 0, (3, 2))
+            sc += s1("ev_s1", 0, 1, (1, 0)) + [("ev_kw",)] + s1("ev_s1", 0, 1, (3, 2)) + tpair("ev_t", 0, (1, 0))
+            sc += s1("ev_s1", 1, 1, (1, 0)) + tpair("ev_t", 1, (1, 0)) + s1("ev_s1", 1, 1, (3, 2)) + tpair("ev_t", 2, (1, 0))
+            ve = [("il_g", 0, 0, 0), ("il_g", 0, 0, 1), ("q_e", 0, 0, 0), ("q_g", 0, 0), ("q_e", 0, 0, 1), ("il_g", 1, 0, 0), ("q_e", 0, 1, 0)]
+            ve += [("il_g", 1, 0, 1), ("q_g", 1, 0), ("q_e", 0, 1, 1), ("ev_e", 1, 0, 1), ("il_t", 0, 0), ("q_e", 1, 0), ("il_x", 0)]
+            ve += [("q_e", 1, 1), ("q_x", 0), ("il_g", 0, 1), ("il_t", 1, 0), ("q_g", 0, 1), ("q_kw",)]
+            ve += [("il_g", 1, 1), ("q_f", 0, 0), ("q_g", 1, 1), ("il_t", 0, 1), ("q_f", 0, 1), ("il_x", 1), ("q_t", 0)]
+            ve += [("q_f", 1, 0), ("il_t", 1, 1), ("q_x", 1)]
+            for j in range(4, 8):
+                n, kv = divmod(j, 2)
+                te += s1("mm_s1", n, kv, (0, 1)) + dxs("mm_dx", j - 4, (0, 1)) + s1("mm_s1", n, kv, (2, 3))
+                te += (half("mm_o1", 2 * j - 10) + half("mm_o1", 2 * j - 9) if 4 < j < 7 else []) + tpair("tr_d", j - 1, (0, 1))
+                sc += s1("ev_s1", n, kv, (1, 0)) + dxs("ev_dx", j - 4, (1, 0)) + s1("ev_s1", n, kv, (3, 2)) + tpair("ev_t", j - 1, (1, 0))
+            ve += [("il_x", 2), ("q_t", 1), ("q_f", 1, 1), ("q_x", 2), ("il_t", 2, 0), ("il_x", 3), ("q_f", 2, 0)]
+            ve += [("il_t", 2, 1), ("q_x", 3), ("q_t", 2), ("q_f", 2, 1), ("il_t", 3, 0)]
+            te += half("mm_o1", 4) + dxs("mm_dx", 4, (0, 1)) + tpair("tr_d", 7, (0, 1)) + half("mm_o1", 5) + dxs("mm_dx", 5, (0, 1))
+            te += dxs("mm_dx", 6, (0, 1)) + half("mm_o1", 6) + half("mm_o1", 7) + dxs("mm_dx", 7, (0, 1))
+            sc += dxs("ev_dx", 4, (1, 0)) + tpair("ev_t", 7, (1, 0)) + dxs("ev_dx", 5, (0, 1)) + dxs("ev_dx", 6, (0,)) + [("ev_o1", 0)] + dxs("ev_dx", 7, (0,))
+            ve += [("il_t", 3, 1), ("q_f", 3, 0), ("q_t", 3, 0), ("q_t", 3, 1), ("q_f", 3, 1)] + dxs("ev_dx", 6, (1,)) + [("ev_o1", 1)] + dxs("ev_dx", 7, (1,))
+            write_in_order({"T": te, "S": sc, "V": ve})

@@ -33,8 +33,8 @@ def tile_efficientspatialwindowattention_pa_v_kernel(
         rot = ctx.enter_context(tc.tile_pool(name="rot", bufs=2))
         psum = ctx.enter_context(tc.psum_pool(name="psum", bufs=1))
 
-        def kept(width, dtype, name):
-            return keep.tile([128, width], dtype, name=name, align_bytes=64)
+        def kept(width, dtype, name, on=None):
+            return keep.tile([128, width], dtype, name=name, tag=on or name, align_bytes=64)
 
         ident = kept(128, F32, "ident")
         e_raw, e_in, e_codes, e_scales = {}, {}, {}, {}
@@ -59,8 +59,9 @@ def tile_efficientspatialwindowattention_pa_v_kernel(
         kw_codes = kept(768, U32, "kw_codes")
         kw_scales = kept(768, U8, "kw_scales")
 
-        d, banks, f_in, f_codes, f_scales, t_in, dx, o1 = {}, {}, {}, {}, {}, {}, {}, {}
+        d, banks, f_in, f_codes, f_scales, t_in, dx, o1, res = {}, {}, {}, {}, {}, {}, {}, {}, {}
         taken = []
+        spent = ["e_in_%d%d" % key for key in e_codes] + ["g_in_%d%d" % key for key in g_codes]
 
         def next_bank(key, tag=None):
             if tag is None:
@@ -69,14 +70,16 @@ def tile_efficientspatialwindowattention_pa_v_kernel(
             banks[key] = psum.tile([128, 512], F32, name="bank", tag=tag)
             return banks[key]
 
-        def load_e(kv, h, tp):
-            src = es[kv].rearrange("(h p tp t) j -> h tp p (t j)", h=2, tp=2, t=2)
-            nc.sync.dma_start(out=e_raw[kv, h, tp][:], in_=src[h, tp])
+        def load_e(kv, h, tp, t=None):
+            src = es[kv].rearrange("(h p tp t) j -> h tp p (t j)", h=2, tp=2, t=2)[h, tp]
+            cols = slice(0, 1024) if t is None else slice(512 * t, 512 * t + 512)
+            nc.sync.dma_start(out=e_raw[kv, h, tp][:, cols], in_=src[:, cols])
 
-        def load_g(kv, w):
-            src = grads[kv].rearrange("w h (p j) d -> w p h (j d)", j=4)
-            dst = g_raw[kv, w // 2][:, 1024 * (w % 2) : 1024 * (w % 2) + 1024]
-            nc.sync.dma_start(out=dst.rearrange("p (h f) -> p h f", h=4), in_=src[w])
+        def load_g(kv, a, b=None):
+            src = grads[kv].rearrange("(a b) h (p j) d -> a p (b h) (j d)", b=2, j=4)[a]
+            dst = g_raw[kv, a][:].rearrange("p (s f) -> p s f", s=8)
+            part = slice(0, 8) if b is None else slice(4 * b, 4 * b + 4)
+            nc.sync.dma_start(out=dst[:, part, :], in_=src[:, part, :])
 
         def load_x(n, b):
             nc.sync.dma_start(out=x_raw[n][:, 1024 * b : 1024 * b + 1024], in_=x_view[n // 2, b, n % 2, 0])
@@ -92,31 +95,37 @@ def tile_efficientspatialwindowattention_pa_v_kernel(
             else:
                 nc.scalar.copy(out=out, in_=in_)
 
-        def transpose_rows(raw, key, tag):
-            bank = next_bank(key, tag)
-            for t in range(2):
+        def transpose_rows(raw, key, rows):
+            bank = next_bank(key)
+            for s, t in enumerate(rows):
                 words = raw[:, 512 * t : 512 * t + 512].bitcast(F32)
                 for u in range(2):
-                    c0 = (2 * t + u) * 128
+                    c0 = (2 * s + u) * 128
                     nc.tensor.transpose(bank[:, c0 : c0 + 128], words[:, u::2], ident[:])
 
-        def join_halves(eng, dst, key):
+        def join_halves(eng, dst, key, rows=2):
             copy(
                 eng,
-                dst.bitcast(F32).rearrange("p (t r u) -> p t r u", t=2, u=2),
-                banks[key][:].rearrange("p (t u r) -> p t r u", t=2, u=2),
+                dst.bitcast(F32).rearrange("p (t r u) -> p t r u", t=rows, u=2),
+                banks[key][:, 0 : 256 * rows].rearrange("p (t u r) -> p t r u", t=rows, u=2),
             )
 
-        def tr_e(kv, h, tp, tag=None):
-            transpose_rows(e_raw[kv, h, tp], ("e", kv, h, tp), tag)
+        def tr_e(kv, h, tp, t=None):
+            transpose_rows(e_raw[kv, h, tp], ("e", kv, h, tp, t), range(2) if t is None else [t])
 
-        def ev_e(eng, kv, h, tp):
+        def ev_e(eng, kv, h, tp, t=None):
             if (kv, h) not in e_in:
-                e_in[kv, h] = rot.tile([128, 2048], BF16, name="e_in", align_bytes=64)
-            join_halves(eng, e_in[kv, h][:, 1024 * tp : 1024 * tp + 1024], ("e", kv, h, tp))
+                e_in[kv, h] = kept(2048, BF16, "e_in_%d%d" % (kv, h))
+            if t is None:
+                join_halves(eng, e_in[kv, h][:, 1024 * tp : 1024 * tp + 1024], ("e", kv, h, tp, t))
+            else:
+                lo = 1024 * tp + 512 * t
+                join_halves(eng, e_in[kv, h][:, lo : lo + 512], ("e", kv, h, tp, t), 1)
 
-        def q_e(kv, h, tp=None):
+        def q_e(kv, h, tp=None, t=None):
             lo, hi = (0, 512) if tp is None else (256 * tp, 256 * tp + 256)
+            if t is not None:
+                lo, hi = lo + 128 * t, lo + 128 * t + 128
             nc.vector.quantize_mx(
                 out=e_codes[kv, h][:, lo:hi].bitcast(E4M3),
                 scales=e_scales[kv, h][:, lo:hi],
@@ -125,7 +134,7 @@ def tile_efficientspatialwindowattention_pa_v_kernel(
 
         def il_g(eng, kv, a, b=None):
             if (kv, a) not in g_in:
-                g_in[kv, a] = rot.tile([128, 2048], BF16, name="g_in", align_bytes=64)
+                g_in[kv, a] = kept(2048, BF16, "g_in_%d%d" % (kv, a))
             cols = slice(0, 2048) if b is None else slice(1024 * b, 1024 * b + 1024)
             copy(
                 eng,
@@ -141,8 +150,8 @@ def tile_efficientspatialwindowattention_pa_v_kernel(
                 in_=g_in[kv, a][:, 4 * lo : 4 * hi],
             )
 
-        def tr_kw(tag=None):
-            transpose_rows(kw_raw, "kw", tag)
+        def tr_kw():
+            transpose_rows(kw_raw, "kw", range(2))
 
         def ev_kw(eng):
             join_halves(eng, kw_in[:], "kw")
@@ -153,7 +162,7 @@ def tile_efficientspatialwindowattention_pa_v_kernel(
             )
 
         def il_x(eng, n):
-            x_in[n] = rot.tile([128, 2048], BF16, name="x_in", align_bytes=64)
+            x_in[n] = kept(2048, BF16, "x_in_%d" % n)
             copy(
                 eng,
                 x_in[n][:].rearrange("p (b c i t) -> p b c t i", b=2, i=4, t=4),
@@ -195,54 +204,93 @@ def tile_efficientspatialwindowattention_pa_v_kernel(
                 f_in[n, t // 2] = rot.tile([128, 2048], BF16, name="f_in", bufs=3, align_bytes=64)
             join_halves(eng, f_in[n, t // 2][:, 1024 * (t % 2) : 1024 * (t % 2) + 1024], ("t", n, t))
 
-        def q_f(n, tp):
-            f_codes[n, tp] = rot.tile([128, 512], U32, name="f_codes", bufs=8, align_bytes=64)
-            f_scales[n, tp] = rot.tile([128, 512], U8, name="f_scales", bufs=8, align_bytes=64)
+        def q_f(n, tp, t=None):
+            if (n, tp) not in f_codes:
+                f_codes[n, tp] = rot.tile([128, 512], U32, name="f_codes", bufs=8, align_bytes=64)
+                f_scales[n, tp] = rot.tile([128, 512], U8, name="f_scales", bufs=8, align_bytes=64)
+            lo, hi = (0, 512) if t is None else (256 * t, 256 * t + 256)
             nc.vector.quantize_mx(
-                out=f_codes[n, tp][:].bitcast(E5M2), scales=f_scales[n, tp][:], in_=f_in[n, tp][:]
+                out=f_codes[n, tp][:, lo:hi].bitcast(E5M2),
+                scales=f_scales[n, tp][:, lo:hi],
+                in_=f_in[n, tp][:, 4 * lo : 4 * hi],
             )
 
-        def mm_dx(n, tp, b):
-            bank = next_bank(("dx", n, tp, b))
-            for t in range(2):
+        def dx_passes(key, n, tp, tiles):
+            bank = next_bank(key)
+            for s, (t, b) in enumerate(tiles):
                 cols = slice((2 * t + b) * 128, (2 * t + b) * 128 + 128)
-                win = slice(256, 768) if t == 0 else slice(0, 512)
+                win = slice(256, 768) if s == 0 else slice(0, 512)
                 nc.tensor.matmul_mx(
                     out=bank[:],
                     lhsT=f_codes[n, tp][:, cols].bitcast(E5M2),
                     lhsT_scale=f_scales[n, tp][:, cols],
                     rhs=kw_codes[:, win].bitcast(E4M3),
                     rhs_scale=kw_scales[:, win],
-                    start=(t == 0),
-                    stop=(t == 1),
+                    start=(s == 0),
+                    stop=(s == len(tiles) - 1),
                 )
 
-        def ev_dx(eng, n, tp, b):
-            dx[n, tp, b] = rot.tile([128, 512], F32, name="dx", bufs=6, align_bytes=64)
-            copy(eng, dx[n, tp, b][:], banks["dx", n, tp, b][:])
+        def dx_tile(n, tp):
+            if (n, tp) not in dx:
+                dx[n, tp] = kept(1024, F32, "dx", spent[2 * n + tp])
+            return dx[n, tp]
+
+        def store_dx(n, tp, b, lo, hi):
             nc.sync.dma_start(
-                out=dx_view[n // 2, b, n % 2, 0][:, :, 512 * tp : 512 * tp + 512], in_=dx[n, tp, b][:]
+                out=dx_view[n // 2, b, n % 2, 0][:, :, 512 * tp + lo : 512 * tp + hi],
+                in_=dx[n, tp][:, 512 * b + lo : 512 * b + hi],
             )
 
-        def il_t(eng, n, kv):
+        def mm_dx(n, tp, b):
+            dx_passes(("dx", n, tp, b), n, tp, [(0, b), (1, b)])
+
+        def ev_dx(eng, n, tp, b):
+            copy(eng, dx_tile(n, tp)[:, 512 * b : 512 * b + 512], banks["dx", n, tp, b][:])
+
+        def mm_dt(n, tp, t):
+            dx_passes(("dt", n, tp, t), n, tp, [(t, 0), (t, 1)])
+
+        def ev_dt(eng, n, tp, t):
+            dst = dx_tile(n, tp)[:].rearrange("p (b t c) -> p t b c", b=2, t=2)[:, t]
+            copy(eng, dst, banks["dt", n, tp, t][:].rearrange("p (b c) -> p b c", b=2))
+
+        def mm_d1(n, tp, t, b):
+            dx_passes(("d1", n, tp, t, b), n, tp, [(t, b)])
+
+        def ev_d1(eng, n, tp, t, b):
+            lo = 512 * b + 256 * t
+            copy(eng, dx_tile(n, tp)[:, lo : lo + 256], banks["d1", n, tp, t, b][:, 0:256])
+
+        def il_t(eng, n, kv, b=None):
             if n not in t_in:
                 t_in[n] = rot.tile([128, 4096], BF16, name="t_in", align_bytes=64)
+            part = slice(0, 4) if b is None else slice(2 * b, 2 * b + 2)
             copy(
                 eng,
-                t_in[n][:].rearrange("p (s k c i t) -> p k s c t i", s=4, k=2, i=4, t=4)[:, kv],
-                d[n][:].rearrange("p (t s k c i) -> p k s c t i", t=4, s=4, k=2, i=4)[:, kv],
+                t_in[n][:].rearrange("p (s k c i t) -> p k s c t i", s=4, k=2, i=4, t=4)[:, kv, part],
+                d[n][:].rearrange("p (t s k c i) -> p k s c t i", t=4, s=4, k=2, i=4)[:, kv, part],
             )
 
-        def q_t(n, b=None):
+        def quantize_t(n, lo, hi):
             if n not in t_codes:
                 t_codes[n] = rot.tile([128, 1024], U32, name="t_codes", bufs=3, align_bytes=64)
                 t_scales[n] = rot.tile([128, 1024], U8, name="t_scales", bufs=3, align_bytes=64)
-            lo, hi = (0, 1024) if b is None else (512 * b, 512 * b + 512)
             nc.vector.quantize_mx(
                 out=t_codes[n][:, lo:hi].bitcast(E5M2),
                 scales=t_scales[n][:, lo:hi],
                 in_=t_in[n][:, 4 * lo : 4 * hi],
             )
+
+        def q_t(n, b=None):
+            if b is None:
+                quantize_t(n, 0, 1024)
+            else:
+                quantize_t(n, 512 * b, 512 * b + 512)
+
+        def q_tk(n, b, kv):
+            for u in range(2):
+                lo = 512 * b + 256 * u + 128 * kv
+                quantize_t(n, lo, lo + 128)
 
         def mm_o1(n, b):
             for m in range(2):
@@ -261,37 +309,42 @@ def tile_efficientspatialwindowattention_pa_v_kernel(
                 )
 
         def ev_o1(eng, m):
-            res = kept(512, F32, "res_%d" % m)
+            res[m] = kept(512, F32, "res_%d" % m)
             copy(
                 eng,
-                res[:].rearrange("p (i u e) -> p i u e", u=2, e=2),
+                res[m][:].rearrange("p (i u e) -> p i u e", u=2, e=2),
                 o1[m][:].rearrange("p (u i e) -> p i u e", u=2, e=2),
             )
-            nc.sync.dma_start(out=out_1[128 * m : 128 * m + 128, :], in_=res[:])
 
+        def st_o1(m):
+            nc.sync.dma_start(out=out_1[128 * m : 128 * m + 128, :], in_=res[m][:])
+
+        def st_dx(n, tp, b):
+            store_dx(n, tp, b, 0, 512)
+
+        def st_d1(n, tp, t, b):
+            store_dx(n, tp, b, 256 * t, 256 * t + 256)
+
+        FINE = False
 
         def needs(op):
             kind, a = op[0], op[1:]
             if kind == "ev_e":
-                kv, h, tp = a
-                return [("tr_e",) + a] + ([("q_e", 0, h)] if kv else [])
+                return [("tr_e",) + a]
             if kind == "q_e":
-                return [("ev_e",) + a] if len(a) == 3 else [("ev_e",) + a + (tp,) for tp in range(2)]
-            if kind == "il_g":
-                return [("q_g", a[0], 0)] if a[1] else []
+                return [("ev_e",) + a] if len(a) >= 3 else [("ev_e",) + a + (tp,) for tp in range(2)]
             if kind == "q_g":
                 return [("il_g",) + a]
             if kind == "ev_kw":
                 return [("tr_kw",)]
             if kind == "q_kw":
                 return [("ev_kw",)]
-            if kind == "il_x":
-                return [("q_x", a[0] - 2)] if a[0] > 1 else []
             if kind == "q_x":
                 return [("il_x",) + a]
             if kind == "mm_s1":
                 n, kv, t = a
-                return [("q_e", kv, n % 2, t // 2), ("q_g", kv, n // 2)]
+                first = (t,) if (kv, n, t // 2) == (0, 0, 0) and FINE else ()
+                return [("q_e", kv, n % 2, t // 2) + first, ("q_g", kv, n // 2)]
             if kind == "ev_s1":
                 return [("mm_s1",) + a]
             if kind == "tr_d":
@@ -302,14 +355,21 @@ def tile_efficientspatialwindowattention_pa_v_kernel(
                 f = 2 * n + t // 2 - 3
                 return [("tr_d",) + a] + ([("q_f", f // 2, f % 2)] if f >= 0 else [])
             if kind == "q_f":
-                n, tp = a
-                return [("ev_t", n, 2 * tp), ("ev_t", n, 2 * tp + 1)]
+                return [("ev_t", a[0], 2 * a[1] + t) for t in (a[2:] or range(2))]
             if kind == "mm_dx":
                 return [("q_f", a[0], a[1]), ("q_kw",)]
-            if kind == "ev_dx":
-                return [("mm_dx",) + a]
+            if kind in ("mm_dt", "mm_d1"):
+                return [("q_f",) + a[:3], ("q_kw",)]
+            if kind in ("ev_dx", "ev_dt", "ev_d1"):
+                return [("mm" + kind[2:],) + a]
+            if kind in ("st_dx", "st_o1"):
+                return [("ev" + kind[2:],) + a]
+            if kind == "st_d1":
+                return [("ev_d1",) + a]
+            if kind == "q_tk":
+                return [("il_t", a[0], a[2], a[1]), ("mm_o1", a[0] - 3, 1)]
             if kind == "il_t":
-                n, kv = a
+                n, kv = a[:2]
                 old = [("q_t", n - 2, b) for b in range(2)] if n > 1 else []
                 return [("ev_s1", n, kv, t) for t in range(4)] + old
             if kind == "q_t":
@@ -326,10 +386,12 @@ def tile_efficientspatialwindowattention_pa_v_kernel(
             "tr_e": tr_e, "ev_e": ev_e, "q_e": q_e, "il_g": il_g, "q_g": q_g, "tr_kw": tr_kw, "ev_kw": ev_kw,
             "q_kw": q_kw, "il_x": il_x, "q_x": q_x, "mm_s1": mm_s1, "ev_s1": ev_s1, "tr_d": tr_d, "ev_t": ev_t,
             "q_f": q_f, "mm_dx": mm_dx, "ev_dx": ev_dx, "il_t": il_t, "q_t": q_t, "mm_o1": mm_o1, "ev_o1": ev_o1,
+            "mm_dt": mm_dt, "ev_dt": ev_dt, "mm_d1": mm_d1, "ev_d1": ev_d1, "q_tk": q_tk,
+            "st_dx": st_dx, "st_o1": st_o1, "st_d1": st_d1,
         }
-        emptied_by = {"tr_e": "ev_e", "tr_kw": "ev_kw", "mm_s1": "ev_s1", "tr_d": "ev_t", "mm_dx": "ev_dx"}
+        emptied_by = {"tr_e": "ev_e", "tr_kw": "ev_kw", "mm_s1": "ev_s1", "tr_d": "ev_t", "mm_dx": "ev_dx", "mm_dt": "ev_dt", "mm_d1": "ev_d1"}
 
-        parts = {"q_e": 4, "il_g": 4, "q_g": 4, "q_t": 3}
+        parts = {"q_e": 4, "il_g": 4, "q_g": 4, "q_t": 3, "q_f": 4, "il_t": 4}
 
         def write_in_order(queues):
             fills = [op for op in queues["T"] if op[0] in emptied_by]
@@ -350,9 +412,17 @@ def tile_efficientspatialwindowattention_pa_v_kernel(
                         else:
                             calls[op[0]](*op[1:])
                         written.add(op)
+                        if op[0] == "ev_dt":
+                            written.add(("ev_d1",) + op[1:] + (0,))
+                            written.add(("ev_d1",) + op[1:] + (1,))
+                        if op[0] == "q_tk" and op[:-1] + (1 - op[-1],) in written:
+                            written.add(("q_t",) + op[1:3])
                         if len(op) < parts.get(op[0], 0):
                             written.add(op + (0,))
                             written.add(op + (1,))
+                        elif len(op) == 5 and op[0] == "q_e":
+                            if op[-1] == 1:
+                                written.add(op[:-1])
                         elif op[0] in parts and op[:-1] + (1 - op[-1],) in written:
                             written.add(op[:-1])
                         heads[eng] = heads[eng] + 1
@@ -365,13 +435,13 @@ def tile_efficientspatialwindowattention_pa_v_kernel(
             nc.gpsimd.memset(kw_scales[:].bitcast(U32)[:, 0:64], 0)
             nc.gpsimd.memset(kw_scales[:].bitcast(U32)[:, 128:192], 0)
             load_e(0, 0, 0)
-            load_g(0, 0)
-            load_g(0, 1)
+            load_g(0, 0, 0)
+            load_g(0, 0, 1)
             load_e(0, 0, 1)
             load_e(0, 1, 0)
             load_e(0, 1, 1)
-            load_g(1, 0)
-            load_g(1, 1)
+            load_g(1, 0, 0)
+            load_g(1, 0, 1)
             for h in range(2):
                 for tp in range(2):
                     load_e(1, h, tp)
@@ -379,8 +449,7 @@ def tile_efficientspatialwindowattention_pa_v_kernel(
             load_x(0, 1)
             load_kw()
             for kv in range(2):
-                for w in range(2, 4):
-                    load_g(kv, w)
+                load_g(kv, 1)
             for n in range(1, 4):
                 for b in range(2):
                     load_x(n, b)
@@ -421,8 +490,12 @@ def tile_efficientspatialwindowattention_pa_v_kernel(
                 sc += s1("ev_s1", n, kv, (1, 0)) + dxs("ev_dx", j - 4, (1, 0)) + s1("ev_s1", n, kv, (3, 2)) + tpair("ev_t", j - 1, (1, 0))
             ve += [("il_x", 2), ("q_t", 1), ("q_f", 1, 1), ("q_x", 2), ("il_t", 2, 0), ("il_x", 3), ("q_f", 2, 0)]
             ve += [("il_t", 2, 1), ("q_x", 3), ("q_t", 2), ("q_f", 2, 1), ("il_t", 3, 0)]
-            te += half("mm_o1", 4) + dxs("mm_dx", 4, (0, 1)) + tpair("tr_d", 7, (0, 1)) + half("mm_o1", 5) + dxs("mm_dx", 5, (0, 1))
+            te += dxs("mm_dx", 4, (0, 1)) + tpair("tr_d", 7, (0, 1)) + half("mm_o1", 4) + dxs("mm_dx", 5, (0, 1)) + half("mm_o1", 5)
             te += dxs("mm_dx", 6, (0, 1)) + half("mm_o1", 6) + half("mm_o1", 7) + dxs("mm_dx", 7, (0, 1))
             sc += dxs("ev_dx", 4, (1, 0)) + tpair("ev_t", 7, (1, 0)) + dxs("ev_dx", 5, (0, 1)) + dxs("ev_dx", 6, (0,)) + [("ev_o1", 0)] + dxs("ev_dx", 7, (0,))
             ve += [("il_t", 3, 1), ("q_f", 3, 0), ("q_t", 3, 0), ("q_t", 3, 1), ("q_f", 3, 1)] + dxs("ev_dx", 6, (1,)) + [("ev_o1", 1)] + dxs("ev_dx", 7, (1,))
-            write_in_order({"T": te, "S": sc, "V": ve})
+            st = []
+            for f in range(5):
+                st += dxs("st_dx", f, (1, 0))
+            st += dxs("st_dx", 5, (0, 1)) + dxs("st_dx", 6, (0, 1)) + [("st_o1", 0), ("st_o1", 1)] + dxs("st_dx", 7, (0, 1))
+            write_in_order({"T": te, "S": sc, "V": ve, "Q": st})

@@ -24,9 +24,7 @@ def tile_efficientspatialwindowattention_pa_v_kernel(
     x_view = x.rearrange(
         "o (a h r b q t) c -> a b h o r q (t c)", a=2, h=2, r=16, b=2, q=8, t=4
     )
-    dx_view = out_0.rearrange(
-        "o (a h r b q t) c -> a b h o r q (t c)", a=2, h=2, r=16, b=2, q=8, t=4
-    )
+    dx_view = out_0.rearrange("o (n g p t) c -> o n g p (t c)", n=4, g=2, t=4)[0]
 
     with ExitStack() as ctx:
         keep = ctx.enter_context(tc.tile_pool(name="keep", bufs=1))
@@ -161,12 +159,14 @@ def tile_efficientspatialwindowattention_pa_v_kernel(
                 out=kw_codes[:, 256:512].bitcast(E4M3), scales=kw_scales[:, 256:512], in_=kw_in[:]
             )
 
-        def il_x(eng, n):
-            x_in[n] = kept(2048, BF16, "x_in_%d" % n)
+        def il_x(eng, n, b=None):
+            if n not in x_in:
+                x_in[n] = kept(2048, BF16, "x_in_%d" % n)
+            part = slice(0, 2) if b is None else slice(b, b + 1)
             copy(
                 eng,
-                x_in[n][:].rearrange("p (b c i t) -> p b c t i", b=2, i=4, t=4),
-                x_raw[n][:].rearrange("p (b t c i) -> p b c t i", b=2, i=4, t=4),
+                x_in[n][:].rearrange("p (b c i t) -> p b c t i", b=2, i=4, t=4)[:, part],
+                x_raw[n][:].rearrange("p (b t c i) -> p b c t i", b=2, i=4, t=4)[:, part],
             )
 
         def q_x(n):
@@ -200,30 +200,36 @@ def tile_efficientspatialwindowattention_pa_v_kernel(
                 nc.tensor.transpose(bank[:, cols], words[:, cols], ident[:])
 
         def ev_t(eng, n, t):
-            if (n, t // 2) not in f_in:
-                f_in[n, t // 2] = rot.tile([128, 2048], BF16, name="f_in", bufs=3, align_bytes=64)
-            join_halves(eng, f_in[n, t // 2][:, 1024 * (t % 2) : 1024 * (t % 2) + 1024], ("t", n, t))
+            if n not in f_in:
+                f_in[n] = rot.tile([128, 4096], BF16, name="f_in", align_bytes=64)
+            copy(
+                eng,
+                f_in[n][:, 1024 * t : 1024 * t + 1024].bitcast(F32).rearrange("p (r b q u) -> p r b q u", b=2, q=8, u=2),
+                banks["t", n, t][:].rearrange("p (b u r q) -> p r b q u", b=2, q=8, u=2),
+            )
 
-        def q_f(n, tp, t=None):
-            if (n, tp) not in f_codes:
-                f_codes[n, tp] = rot.tile([128, 512], U32, name="f_codes", bufs=8, align_bytes=64)
-                f_scales[n, tp] = rot.tile([128, 512], U8, name="f_scales", bufs=8, align_bytes=64)
-            lo, hi = (0, 512) if t is None else (256 * t, 256 * t + 256)
+        def q_f(n, tp=None, t=None):
+            if n not in f_codes:
+                f_codes[n] = kept(1024, U32, "f_codes_%d" % n)
+                f_scales[n] = kept(1024, U8, "f_scales_%d" % n)
+            lo, hi = (0, 1024) if tp is None else (512 * tp, 512 * tp + 512)
+            if t is not None:
+                lo, hi = lo + 256 * t, lo + 256 * t + 256
             nc.vector.quantize_mx(
-                out=f_codes[n, tp][:, lo:hi].bitcast(E5M2),
-                scales=f_scales[n, tp][:, lo:hi],
-                in_=f_in[n, tp][:, 4 * lo : 4 * hi],
+                out=f_codes[n][:, lo:hi].bitcast(E5M2),
+                scales=f_scales[n][:, lo:hi],
+                in_=f_in[n][:, 4 * lo : 4 * hi],
             )
 
         def dx_passes(key, n, tp, tiles):
             bank = next_bank(key)
             for s, (t, b) in enumerate(tiles):
-                cols = slice((2 * t + b) * 128, (2 * t + b) * 128 + 128)
+                cols = slice((4 * tp + 2 * t + b) * 128, (4 * tp + 2 * t + b) * 128 + 128)
                 win = slice(256, 768) if s == 0 else slice(0, 512)
                 nc.tensor.matmul_mx(
                     out=bank[:],
-                    lhsT=f_codes[n, tp][:, cols].bitcast(E5M2),
-                    lhsT_scale=f_scales[n, tp][:, cols],
+                    lhsT=f_codes[n][:, cols].bitcast(E5M2),
+                    lhsT_scale=f_scales[n][:, cols],
                     rhs=kw_codes[:, win].bitcast(E4M3),
                     rhs_scale=kw_scales[:, win],
                     start=(s == 0),
@@ -237,7 +243,7 @@ def tile_efficientspatialwindowattention_pa_v_kernel(
 
         def store_dx(n, tp, b, lo, hi):
             nc.sync.dma_start(
-                out=dx_view[n // 2, b, n % 2, 0][:, :, 512 * tp + lo : 512 * tp + hi],
+                out=dx_view[n, b][:, 512 * tp + lo : 512 * tp + hi],
                 in_=dx[n, tp][:, 512 * b + lo : 512 * b + hi],
             )
 
@@ -352,9 +358,10 @@ def tile_efficientspatialwindowattention_pa_v_kernel(
                 return [("ev_s1", n, 0, t), ("ev_s1", n, 1, t)]
             if kind == "ev_t":
                 n, t = a
-                f = 2 * n + t // 2 - 3
-                return [("tr_d",) + a] + ([("q_f", f // 2, f % 2)] if f >= 0 else [])
+                return [("tr_d",) + a] + ([("q_f", n - 2, tp) for tp in range(2)] if n > 1 else [])
             if kind == "q_f":
+                if len(a) == 1:
+                    return [("ev_t", a[0], t) for t in range(4)]
                 return [("ev_t", a[0], 2 * a[1] + t) for t in (a[2:] or range(2))]
             if kind == "mm_dx":
                 return [("q_f", a[0], a[1]), ("q_kw",)]
@@ -391,7 +398,7 @@ def tile_efficientspatialwindowattention_pa_v_kernel(
         }
         emptied_by = {"tr_e": "ev_e", "tr_kw": "ev_kw", "mm_s1": "ev_s1", "tr_d": "ev_t", "mm_dx": "ev_dx", "mm_dt": "ev_dt", "mm_d1": "ev_d1"}
 
-        parts = {"q_e": 4, "il_g": 4, "q_g": 4, "q_t": 3, "q_f": 4, "il_t": 4}
+        parts = {"q_e": 4, "il_g": 4, "q_g": 4, "q_t": 3, "q_f": 4, "il_t": 4, "il_x": 3}
 
         def write_in_order(queues):
             fills = [op for op in queues["T"] if op[0] in emptied_by]
@@ -445,12 +452,10 @@ def tile_efficientspatialwindowattention_pa_v_kernel(
             for h in range(2):
                 for tp in range(2):
                     load_e(1, h, tp)
-            load_x(0, 0)
-            load_x(0, 1)
             load_kw()
             for kv in range(2):
                 load_g(kv, 1)
-            for n in range(1, 4):
+            for n in range(4):
                 for b in range(2):
                     load_x(n, b)
 
@@ -479,23 +484,22 @@ def tile_efficientspatialwindowattention_pa_v_kernel(
             sc += s1("ev_s1", 0, 1, (1, 0)) + [("ev_kw",)] + s1("ev_s1", 0, 1, (3, 2)) + tpair("ev_t", 0, (1, 0))
             sc += s1("ev_s1", 1, 1, (1, 0)) + tpair("ev_t", 1, (1, 0)) + s1("ev_s1", 1, 1, (3, 2)) + tpair("ev_t", 2, (1, 0))
             ve = [("il_g", 0, 0, 0), ("il_g", 0, 0, 1), ("q_e", 0, 0, 0), ("q_g", 0, 0), ("q_e", 0, 0, 1), ("il_g", 1, 0, 0), ("q_e", 0, 1, 0)]
-            ve += [("il_g", 1, 0, 1), ("q_g", 1, 0), ("q_e", 0, 1, 1), ("ev_e", 1, 0, 1), ("il_t", 0, 0), ("q_e", 1, 0), ("il_x", 0)]
-            ve += [("q_e", 1, 1), ("q_x", 0), ("il_g", 0, 1), ("il_t", 1, 0), ("q_g", 0, 1), ("q_kw",)]
-            ve += [("il_g", 1, 1), ("q_f", 0, 0), ("q_g", 1, 1), ("il_t", 0, 1), ("q_f", 0, 1), ("il_x", 1), ("q_t", 0)]
+            ve += [("il_g", 1, 0, 1), ("q_g", 1, 0), ("q_e", 0, 1, 1), ("ev_e", 1, 0, 1), ("il_t", 0, 0), ("q_e", 1, 0), ("il_g", 0, 1)]
+            ve += [("q_e", 1, 1), ("il_g", 1, 1), ("q_g", 0, 1), ("il_t", 1, 0), ("q_g", 1, 1), ("q_kw",)]
+            ve += [("il_x", 0), ("q_f", 0, 0), ("q_x", 0), ("il_t", 0, 1), ("q_f", 0, 1), ("il_x", 1), ("q_t", 0)]
             ve += [("q_f", 1, 0), ("il_t", 1, 1), ("q_x", 1)]
             for j in range(4, 8):
                 n, kv = divmod(j, 2)
                 te += s1("mm_s1", n, kv, (0, 1)) + dxs("mm_dx", j - 4, (0, 1)) + s1("mm_s1", n, kv, (2, 3))
-                te += (half("mm_o1", 2 * j - 10) + half("mm_o1", 2 * j - 9) if 4 < j < 7 else []) + tpair("tr_d", j - 1, (0, 1))
+                te += (half("mm_o1", 2 * j - 10) + half("mm_o1", 2 * j - 9) if 4 < j else []) + tpair("tr_d", j - 1, (0, 1))
                 sc += s1("ev_s1", n, kv, (1, 0)) + dxs("ev_dx", j - 4, (1, 0)) + s1("ev_s1", n, kv, (3, 2)) + tpair("ev_t", j - 1, (1, 0))
-            ve += [("il_x", 2), ("q_t", 1), ("q_f", 1, 1), ("q_x", 2), ("il_t", 2, 0), ("il_x", 3), ("q_f", 2, 0)]
-            ve += [("il_t", 2, 1), ("q_x", 3), ("q_t", 2), ("q_f", 2, 1), ("il_t", 3, 0)]
-            te += dxs("mm_dx", 4, (0, 1)) + tpair("tr_d", 7, (0, 1)) + half("mm_o1", 4) + dxs("mm_dx", 5, (0, 1)) + half("mm_o1", 5)
-            te += dxs("mm_dx", 6, (0, 1)) + half("mm_o1", 6) + half("mm_o1", 7) + dxs("mm_dx", 7, (0, 1))
-            sc += dxs("ev_dx", 4, (1, 0)) + tpair("ev_t", 7, (1, 0)) + dxs("ev_dx", 5, (0, 1)) + dxs("ev_dx", 6, (0,)) + [("ev_o1", 0)] + dxs("ev_dx", 7, (0,))
-            ve += [("il_t", 3, 1), ("q_f", 3, 0), ("q_t", 3, 0), ("q_t", 3, 1), ("q_f", 3, 1)] + dxs("ev_dx", 6, (1,)) + [("ev_o1", 1)] + dxs("ev_dx", 7, (1,))
+            ve += [("il_x", 2), ("q_t", 1), ("q_f", 1, 1), ("q_x", 2), ("il_t", 2, 0), ("il_t", 2, 1), ("q_f", 2, 0)]
+            ve += [("q_t", 2), ("il_x", 3), ("q_f", 2, 1), ("il_t", 3, 0), ("q_x", 3)]
+            te += dxs("mm_dx", 4, (0, 1)) + dxs("mm_dx", 5, (0, 1)) + tpair("tr_d", 7, (0, 1)) + dxs("mm_dx", 6, (0, 1)) + half("mm_o1", 6) + half("mm_o1", 7) + dxs("mm_dx", 7, (0, 1))
+            sc += dxs("ev_dx", 4, (1, 0)) + dxs("ev_dx", 5, (1,)) + tpair("ev_t", 7, (1, 0)) + dxs("ev_dx", 6, (0,1)) + [("ev_o1", 0)] + dxs("ev_dx", 7, (0,))
+            ve += [("il_t", 3, 1), ("q_f", 3, 0), ("ev_dx", 2, 1, 0), ("q_t", 3, 0), ("q_t", 3, 1), ("q_f", 3, 1)] + [("ev_o1", 1)] + dxs("ev_dx", 7, (1,))
             st = []
             for f in range(5):
                 st += dxs("st_dx", f, (1, 0))
-            st += dxs("st_dx", 5, (0, 1)) + dxs("st_dx", 6, (0, 1)) + [("st_o1", 0), ("st_o1", 1)] + dxs("st_dx", 7, (0, 1))
+            st += dxs("st_dx", 5, (1, 0)) + dxs("st_dx", 6, (0, 1)) + [("st_o1", 0), ("st_o1", 1)] + dxs("st_dx", 7, (0, 1))
             write_in_order({"T": te, "S": sc, "V": ve, "Q": st})

@@ -13,6 +13,7 @@ E5M2 = mybir.dt.float8_e5m2_x4
 FLOPS = 2 * 2 * 4 * 1024 * 512 * 256 + 2 * 2 * 4096 * 512 * 256
 
 ROTATING_BANKS = 6
+DX_LAG = 4
 
 
 def tile_efficientspatialwindowattention_pa_v_kernel(
@@ -21,9 +22,7 @@ def tile_efficientspatialwindowattention_pa_v_kernel(
     nc = tc.nc
     es = (e_k, e_v)
     grads = (grad_0, grad_1)
-    x_view = x.rearrange(
-        "o (a h r b q t) c -> a b h o r q (t c)", a=2, h=2, r=16, b=2, q=8, t=4
-    )
+    x_view = x.rearrange("o (a h r b q t) c -> a b h o r q (t c)", a=2, h=2, r=16, b=2, q=8, t=4)
     dx_view = out_0.rearrange("o (n g p t) c -> o n g p (t c)", n=4, g=2, t=4)[0]
 
     with ExitStack() as ctx:
@@ -47,7 +46,7 @@ def tile_efficientspatialwindowattention_pa_v_kernel(
                 g_raw[kv, a] = kept(2048, BF16, "g_raw_%d%d" % (kv, a))
                 g_codes[kv, a] = kept(512, U32, "g_codes_%d%d" % (kv, a))
                 g_scales[kv, a] = kept(512, U8, "g_scales_%d%d" % (kv, a))
-        x_raw, x_in, x_codes, x_scales, t_codes, t_scales = {}, {}, {}, {}, {}, {}
+        x_raw, x_in, x_codes, x_scales = {}, {}, {}, {}
         for n in range(4):
             x_raw[n] = kept(2048, BF16, "x_raw_%d" % n)
             x_codes[n] = kept(512, U32, "x_codes_%d" % n)
@@ -57,27 +56,39 @@ def tile_efficientspatialwindowattention_pa_v_kernel(
         kw_codes = kept(768, U32, "kw_codes")
         kw_scales = kept(768, U8, "kw_scales")
 
-        d, banks, f_in, f_codes, f_scales, t_in, dx, o1, res = {}, {}, {}, {}, {}, {}, {}, {}, {}
-        taken = []
+        dkv, tok_in, tok_codes, tok_scales, col_in, col_codes, col_scales = {}, {}, {}, {}, {}, {}, {}
+        banks, dx, dw_banks, dw = {}, {}, {}, {}
         spent = ["e_in_%d%d" % key for key in e_codes] + ["g_in_%d%d" % key for key in g_codes]
 
-        def next_bank(key, tag=None):
-            if tag is None:
-                tag = "bank_%d" % (len(taken) % ROTATING_BANKS)
-                taken.append(key)
+        def next_bank(key):
+            tag = "bank_%d" % (len(banks) % ROTATING_BANKS)
             banks[key] = psum.tile([128, 512], F32, name="bank", tag=tag)
             return banks[key]
 
-        def load_e(kv, h, tp, t=None):
-            src = es[kv].rearrange("(h p tp t) j -> h tp p (t j)", h=2, tp=2, t=2)[h, tp]
-            cols = slice(0, 1024) if t is None else slice(512 * t, 512 * t + 512)
-            nc.sync.dma_start(out=e_raw[kv, h, tp][:, cols], in_=src[:, cols])
+        def copy(eng, out, in_):
+            if eng == "vector":
+                nc.vector.tensor_copy(out=out, in_=in_)
+            else:
+                nc.scalar.copy(out=out, in_=in_)
+
+        def quantize(codes, scales, values, fmt, lo, hi):
+            nc.vector.quantize_mx(
+                out=codes[:, lo:hi].bitcast(fmt), scales=scales[:, lo:hi], in_=values[:, 4 * lo : 4 * hi]
+            )
+
+        def span(part, width):
+            return (0, width) if part is None else (part * width // 2, (part + 1) * width // 2)
+
+
+        def load_e(kv, h, tp):
+            src = es[kv].rearrange("(h p tp t) j -> h tp p (t j)", h=2, tp=2, t=2)
+            nc.sync.dma_start(out=e_raw[kv, h, tp][:], in_=src[h, tp])
 
         def load_g(kv, a, b=None):
             src = grads[kv].rearrange("(a b) h (p j) d -> a p (b h) (j d)", b=2, j=4)[a]
             dst = g_raw[kv, a][:].rearrange("p (s f) -> p s f", s=8)
-            part = slice(0, 8) if b is None else slice(4 * b, 4 * b + 4)
-            nc.sync.dma_start(out=dst[:, part, :], in_=src[:, part, :])
+            lo, hi = span(b, 8)
+            nc.sync.dma_start(out=dst[:, lo:hi, :], in_=src[:, lo:hi, :])
 
         def load_x(n, b):
             nc.sync.dma_start(out=x_raw[n][:, 1024 * b : 1024 * b + 1024], in_=x_view[n // 2, b, n % 2, 0])
@@ -87,353 +98,310 @@ def tile_efficientspatialwindowattention_pa_v_kernel(
                 out=kw_raw[:].rearrange("p (m k) -> p m k", m=2), in_=kv_w.rearrange("(m p) k -> p m k", m=2)
             )
 
-        def copy(eng, out, in_):
-            if eng == "V":
-                nc.vector.tensor_copy(out=out, in_=in_)
-            else:
-                nc.scalar.copy(out=out, in_=in_)
+        def store_dx(f, g):
+            n, tp = divmod(f, 2)
+            nc.sync.dma_start(
+                out=dx_view[n, g][:, 512 * tp : 512 * tp + 512], in_=dx[f][:, 512 * g : 512 * g + 512]
+            )
 
-        def transpose_rows(raw, key, rows):
+        def store_dw(m):
+            nc.sync.dma_start(out=out_1[128 * m : 128 * m + 128, :], in_=dw[m][:])
+
+
+        def transpose_rows(raw, key):
             bank = next_bank(key)
-            for s, t in enumerate(rows):
-                words = raw[:, 512 * t : 512 * t + 512].bitcast(F32)
+            for row in range(2):
+                words = raw[:, 512 * row : 512 * row + 512].bitcast(F32)
                 for u in range(2):
-                    c0 = (2 * s + u) * 128
+                    c0 = (2 * row + u) * 128
                     nc.tensor.transpose(bank[:, c0 : c0 + 128], words[:, u::2], ident[:])
 
-        def join_halves(eng, dst, key, rows=2):
+        def join_words(eng, dst, key):
             copy(
                 eng,
-                dst.bitcast(F32).rearrange("p (t r u) -> p t r u", t=rows, u=2),
-                banks[key][:, 0 : 256 * rows].rearrange("p (t u r) -> p t r u", t=rows, u=2),
+                dst.bitcast(F32).rearrange("p (row c u) -> p row c u", row=2, u=2),
+                banks[key][:].rearrange("p (row u c) -> p row c u", row=2, u=2),
             )
 
-        def tr_e(kv, h, tp, t=None):
-            transpose_rows(e_raw[kv, h, tp], ("e", kv, h, tp, t), range(2) if t is None else [t])
+        def turn_e(kv, h, tp):
+            transpose_rows(e_raw[kv, h, tp], ("e", kv, h, tp))
 
-        def ev_e(eng, kv, h, tp, t=None):
+        def take_e(eng, kv, h, tp):
             if (kv, h) not in e_in:
                 e_in[kv, h] = kept(2048, BF16, "e_in_%d%d" % (kv, h))
-            if t is None:
-                join_halves(eng, e_in[kv, h][:, 1024 * tp : 1024 * tp + 1024], ("e", kv, h, tp, t))
-            else:
-                lo = 1024 * tp + 512 * t
-                join_halves(eng, e_in[kv, h][:, lo : lo + 512], ("e", kv, h, tp, t), 1)
+            join_words(eng, e_in[kv, h][:, 1024 * tp : 1024 * tp + 1024], ("e", kv, h, tp))
 
-        def q_e(kv, h, tp=None, t=None):
-            lo, hi = (0, 512) if tp is None else (256 * tp, 256 * tp + 256)
-            if t is not None:
-                lo, hi = lo + 128 * t, lo + 128 * t + 128
-            nc.vector.quantize_mx(
-                out=e_codes[kv, h][:, lo:hi].bitcast(E4M3),
-                scales=e_scales[kv, h][:, lo:hi],
-                in_=e_in[kv, h][:, 4 * lo : 4 * hi],
-            )
+        def quant_e(kv, h, tp=None):
+            quantize(e_codes[kv, h], e_scales[kv, h], e_in[kv, h], E4M3, *span(tp, 512))
 
-        def il_g(eng, kv, a, b=None):
-            if (kv, a) not in g_in:
-                g_in[kv, a] = kept(2048, BF16, "g_in_%d%d" % (kv, a))
-            cols = slice(0, 2048) if b is None else slice(1024 * b, 1024 * b + 1024)
-            copy(
-                eng,
-                g_in[kv, a][:, cols].rearrange("p (h d i j) -> p h d j i", d=16, i=4, j=4),
-                g_raw[kv, a][:, cols].rearrange("p (h j d i) -> p h d j i", d=16, j=4, i=4),
-            )
+        def turn_kw():
+            transpose_rows(kw_raw, "kw")
 
-        def q_g(kv, a, b=None):
-            lo, hi = (0, 512) if b is None else (256 * b, 256 * b + 256)
-            nc.vector.quantize_mx(
-                out=g_codes[kv, a][:, lo:hi].bitcast(E5M2),
-                scales=g_scales[kv, a][:, lo:hi],
-                in_=g_in[kv, a][:, 4 * lo : 4 * hi],
-            )
+        def take_kw(eng):
+            join_words(eng, kw_in[:], "kw")
 
-        def tr_kw():
-            transpose_rows(kw_raw, "kw", range(2))
-
-        def ev_kw(eng):
-            join_halves(eng, kw_in[:], "kw")
-
-        def q_kw():
+        def quant_kw():
             nc.vector.quantize_mx(
                 out=kw_codes[:, 256:512].bitcast(E4M3), scales=kw_scales[:, 256:512], in_=kw_in[:]
             )
 
-        def il_x(eng, n, b=None):
-            if n not in x_in:
-                x_in[n] = kept(2048, BF16, "x_in_%d" % n)
-            part = slice(0, 2) if b is None else slice(b, b + 1)
-            copy(
-                eng,
-                x_in[n][:].rearrange("p (b c i t) -> p b c t i", b=2, i=4, t=4)[:, part],
-                x_raw[n][:].rearrange("p (b t c i) -> p b c t i", b=2, i=4, t=4)[:, part],
+
+        def mix_g(kv, a, b=None):
+            if (kv, a) not in g_in:
+                g_in[kv, a] = kept(2048, BF16, "g_in_%d%d" % (kv, a))
+            lo, hi = span(b, 2048)
+            nc.vector.tensor_copy(
+                out=g_in[kv, a][:, lo:hi].rearrange("p (h d i j) -> p h d j i", d=16, i=4, j=4),
+                in_=g_raw[kv, a][:, lo:hi].rearrange("p (h j d i) -> p h d j i", d=16, j=4, i=4),
             )
 
-        def q_x(n):
-            nc.vector.quantize_mx(out=x_codes[n][:].bitcast(E4M3), scales=x_scales[n][:], in_=x_in[n][:])
+        def quant_g(kv, a):
+            quantize(g_codes[kv, a], g_scales[kv, a], g_in[kv, a], E5M2, 0, 512)
 
-        def mm_s1(n, kv, t):
-            h = n % 2
-            bank = next_bank(("s1", n, kv, t))
+        def mix_x(n):
+            x_in[n] = kept(2048, BF16, "x_in_%d" % n)
+            nc.vector.tensor_copy(
+                out=x_in[n][:].rearrange("p (b c i t) -> p b c t i", b=2, i=4, t=4),
+                in_=x_raw[n][:].rearrange("p (b t c i) -> p b c t i", b=2, i=4, t=4),
+            )
+
+        def quant_x(n):
+            quantize(x_codes[n], x_scales[n], x_in[n], E4M3, 0, 512)
+
+
+        def pass_dkv(j, t):
+            n, kv = divmod(j, 2)
             cols = slice(128 * t, 128 * t + 128)
             nc.tensor.matmul_mx(
-                out=bank[:],
-                lhsT=e_codes[kv, h][:, cols].bitcast(E4M3),
-                lhsT_scale=e_scales[kv, h][:, cols],
+                out=next_bank(("dkv", j, t))[:],
+                lhsT=e_codes[kv, n % 2][:, cols].bitcast(E4M3),
+                lhsT_scale=e_scales[kv, n % 2][:, cols],
                 rhs=g_codes[kv, n // 2][:].bitcast(E5M2),
                 rhs_scale=g_scales[kv, n // 2][:],
                 start=True,
                 stop=True,
             )
 
-        def ev_s1(eng, n, kv, t):
-            if n not in d:
-                d[n] = rot.tile([128, 4096], BF16, name="d", bufs=4, align_bytes=64)
-            dst = d[n][:].rearrange("p (t b u k i e) -> p t k b u i e", t=4, b=2, u=2, k=2, e=2)[:, t, kv]
-            copy(eng, dst, banks["s1", n, kv, t][:].rearrange("p (b i u e) -> p b u i e", b=2, u=2, e=2))
+        def take_dkv(eng, j, t):
+            n, kv = divmod(j, 2)
+            if n not in dkv:
+                dkv[n] = rot.tile([128, 4096], BF16, name="dkv", bufs=4, align_bytes=64)
+            dst = dkv[n][:].rearrange("p (t b u k i e) -> p t k b u i e", t=4, b=2, u=2, k=2, e=2)[:, t, kv]
+            copy(eng, dst, banks["dkv", j, t][:].rearrange("p (b i u e) -> p b u i e", b=2, u=2, e=2))
 
-        def tr_d(n, t):
-            bank = next_bank(("t", n, t))
-            words = d[n][:, 1024 * t : 1024 * t + 1024].bitcast(F32)
-            for s in range(4):
-                cols = slice(128 * s, 128 * s + 128)
+
+        def turn_dkv(f, s):
+            n, t = divmod(2 * f + s, 4)
+            bank = next_bank(("col", f, s))
+            words = dkv[n][:, 1024 * t : 1024 * t + 1024].bitcast(F32)
+            for bu in range(4):
+                cols = slice(128 * bu, 128 * bu + 128)
                 nc.tensor.transpose(bank[:, cols], words[:, cols], ident[:])
 
-        def ev_t(eng, n, t):
-            if n not in f_in:
-                f_in[n] = rot.tile([128, 4096], BF16, name="f_in", align_bytes=64)
+        def take_col(eng, f, s):
+            n, t = divmod(2 * f + s, 4)
+            if n not in col_in:
+                col_in[n] = rot.tile([128, 4096], BF16, name="col_in", align_bytes=64)
+            dst = col_in[n][:, 1024 * t : 1024 * t + 1024].bitcast(F32)
             copy(
                 eng,
-                f_in[n][:, 1024 * t : 1024 * t + 1024].bitcast(F32).rearrange("p (r b q u) -> p r b q u", b=2, q=8, u=2),
-                banks["t", n, t][:].rearrange("p (b u r q) -> p r b q u", b=2, q=8, u=2),
+                dst.rearrange("p (r b q u) -> p r b q u", b=2, q=8, u=2),
+                banks["col", f, s][:].rearrange("p (b u r q) -> p r b q u", b=2, q=8, u=2),
             )
 
-        def q_f(n, tp=None, t=None):
-            if n not in f_codes:
-                f_codes[n] = kept(1024, U32, "f_codes_%d" % n)
-                f_scales[n] = kept(1024, U8, "f_scales_%d" % n)
-            lo, hi = (0, 1024) if tp is None else (512 * tp, 512 * tp + 512)
-            if t is not None:
-                lo, hi = lo + 256 * t, lo + 256 * t + 256
-            nc.vector.quantize_mx(
-                out=f_codes[n][:, lo:hi].bitcast(E5M2),
-                scales=f_scales[n][:, lo:hi],
-                in_=f_in[n][:, 4 * lo : 4 * hi],
-            )
+        def quant_col(f):
+            n, tp = divmod(f, 2)
+            if n not in col_codes:
+                col_codes[n] = kept(1024, U32, "col_codes_%d" % n)
+                col_scales[n] = kept(1024, U8, "col_scales_%d" % n)
+            quantize(col_codes[n], col_scales[n], col_in[n], E5M2, *span(tp, 1024))
 
-        def dx_passes(key, n, tp, tiles):
-            bank = next_bank(key)
-            for s, (t, b) in enumerate(tiles):
-                cols = slice((4 * tp + 2 * t + b) * 128, (4 * tp + 2 * t + b) * 128 + 128)
+        def pass_dx(f, g):
+            n, tp = divmod(f, 2)
+            bank = next_bank(("dx", f, g))
+            for s in range(2):
+                c0 = 256 * (2 * tp + s) + 128 * g
                 win = slice(256, 768) if s == 0 else slice(0, 512)
                 nc.tensor.matmul_mx(
                     out=bank[:],
-                    lhsT=f_codes[n][:, cols].bitcast(E5M2),
-                    lhsT_scale=f_scales[n][:, cols],
+                    lhsT=col_codes[n][:, c0 : c0 + 128].bitcast(E5M2),
+                    lhsT_scale=col_scales[n][:, c0 : c0 + 128],
                     rhs=kw_codes[:, win].bitcast(E4M3),
                     rhs_scale=kw_scales[:, win],
                     start=(s == 0),
-                    stop=(s == len(tiles) - 1),
+                    stop=(s == 1),
                 )
 
-        def dx_tile(n, tp):
-            if (n, tp) not in dx:
-                dx[n, tp] = kept(1024, F32, "dx", spent[2 * n + tp])
-            return dx[n, tp]
+        def take_dx(eng, f, g):
+            if f not in dx:
+                dx[f] = kept(1024, F32, "dx", spent[f])
+            copy(eng, dx[f][:, 512 * g : 512 * g + 512], banks["dx", f, g][:])
 
-        def store_dx(n, tp, b, lo, hi):
-            nc.sync.dma_start(
-                out=dx_view[n, b][:, 512 * tp + lo : 512 * tp + hi],
-                in_=dx[n, tp][:, 512 * b + lo : 512 * b + hi],
+
+        def mix_tok(j):
+            n, kv = divmod(j, 2)
+            if n not in tok_in:
+                tok_in[n] = rot.tile([128, 4096], BF16, name="tok_in", align_bytes=64)
+            nc.vector.tensor_copy(
+                out=tok_in[n][:].rearrange("p (bu k c i t) -> p k bu c t i", bu=4, k=2, i=4, t=4)[:, kv],
+                in_=dkv[n][:].rearrange("p (t bu k c i) -> p k bu c t i", t=4, bu=4, k=2, i=4)[:, kv],
             )
 
-        def mm_dx(n, tp, b):
-            dx_passes(("dx", n, tp, b), n, tp, [(0, b), (1, b)])
+        def quant_tok(n, b=None):
+            if n not in tok_codes:
+                tok_codes[n] = rot.tile([128, 1024], U32, name="tok_codes", bufs=3, align_bytes=64)
+                tok_scales[n] = rot.tile([128, 1024], U8, name="tok_scales", bufs=3, align_bytes=64)
+            quantize(tok_codes[n], tok_scales[n], tok_in[n], E5M2, *span(b, 1024))
 
-        def ev_dx(eng, n, tp, b):
-            copy(eng, dx_tile(n, tp)[:, 512 * b : 512 * b + 512], banks["dx", n, tp, b][:])
-
-        def mm_dt(n, tp, t):
-            dx_passes(("dt", n, tp, t), n, tp, [(t, 0), (t, 1)])
-
-        def ev_dt(eng, n, tp, t):
-            dst = dx_tile(n, tp)[:].rearrange("p (b t c) -> p t b c", b=2, t=2)[:, t]
-            copy(eng, dst, banks["dt", n, tp, t][:].rearrange("p (b c) -> p b c", b=2))
-
-        def mm_d1(n, tp, t, b):
-            dx_passes(("d1", n, tp, t, b), n, tp, [(t, b)])
-
-        def ev_d1(eng, n, tp, t, b):
-            lo = 512 * b + 256 * t
-            copy(eng, dx_tile(n, tp)[:, lo : lo + 256], banks["d1", n, tp, t, b][:, 0:256])
-
-        def il_t(eng, n, kv, b=None):
-            if n not in t_in:
-                t_in[n] = rot.tile([128, 4096], BF16, name="t_in", align_bytes=64)
-            part = slice(0, 4) if b is None else slice(2 * b, 2 * b + 2)
-            copy(
-                eng,
-                t_in[n][:].rearrange("p (s k c i t) -> p k s c t i", s=4, k=2, i=4, t=4)[:, kv, part],
-                d[n][:].rearrange("p (t s k c i) -> p k s c t i", t=4, s=4, k=2, i=4)[:, kv, part],
-            )
-
-        def quantize_t(n, lo, hi):
-            if n not in t_codes:
-                t_codes[n] = rot.tile([128, 1024], U32, name="t_codes", bufs=3, align_bytes=64)
-                t_scales[n] = rot.tile([128, 1024], U8, name="t_scales", bufs=3, align_bytes=64)
-            nc.vector.quantize_mx(
-                out=t_codes[n][:, lo:hi].bitcast(E5M2),
-                scales=t_scales[n][:, lo:hi],
-                in_=t_in[n][:, 4 * lo : 4 * hi],
-            )
-
-        def q_t(n, b=None):
-            if b is None:
-                quantize_t(n, 0, 1024)
-            else:
-                quantize_t(n, 512 * b, 512 * b + 512)
-
-        def q_tk(n, b, kv):
-            for u in range(2):
-                lo = 512 * b + 256 * u + 128 * kv
-                quantize_t(n, lo, lo + 128)
-
-        def mm_o1(n, b):
+        def pass_dw(n, b):
             for m in range(2):
-                if m not in o1:
-                    o1[m] = next_bank(("o1", m), "held_%d" % m)
+                if m not in dw_banks:
+                    dw_banks[m] = psum.tile([128, 512], F32, name="held", tag="held_%d" % m)
                 cols = slice(256 * b + 128 * m, 256 * b + 128 * m + 128)
                 win = slice(512 * b, 512 * b + 512)
                 nc.tensor.matmul_mx(
-                    out=o1[m][:],
+                    out=dw_banks[m][:],
                     lhsT=x_codes[n][:, cols].bitcast(E4M3),
                     lhsT_scale=x_scales[n][:, cols],
-                    rhs=t_codes[n][:, win].bitcast(E5M2),
-                    rhs_scale=t_scales[n][:, win],
+                    rhs=tok_codes[n][:, win].bitcast(E5M2),
+                    rhs_scale=tok_scales[n][:, win],
                     start=(n == 0 and b == 0),
                     stop=(n == 3 and b == 1),
                 )
 
-        def ev_o1(eng, m):
-            res[m] = kept(512, F32, "res_%d" % m)
+        def take_dw(eng, m):
+            dw[m] = kept(512, F32, "dw_%d" % m)
             copy(
                 eng,
-                res[m][:].rearrange("p (i u e) -> p i u e", u=2, e=2),
-                o1[m][:].rearrange("p (u i e) -> p i u e", u=2, e=2),
+                dw[m][:].rearrange("p (i u e) -> p i u e", u=2, e=2),
+                dw_banks[m][:].rearrange("p (u i e) -> p i u e", u=2, e=2),
             )
 
-        def st_o1(m):
-            nc.sync.dma_start(out=out_1[128 * m : 128 * m + 128, :], in_=res[m][:])
 
-        def st_dx(n, tp, b):
-            store_dx(n, tp, b, 0, 512)
+        both = (0, 1)
+        indices = {quant_e: 3, mix_g: 3, quant_tok: 2}
+        emptied_by = {turn_e: take_e, turn_kw: take_kw, pass_dkv: take_dkv, turn_dkv: take_col, pass_dx: take_dx}
+        filled_by = {take: fill for fill, take in emptied_by.items()}
 
-        def st_d1(n, tp, t, b):
-            store_dx(n, tp, b, 256 * t, 256 * t + 256)
+        def halves(step):
+            whole = len(step) - 1 < indices.get(step[0], 0)
+            return [step + (s,) for s in both] if whole else [step]
 
-        FINE = False
-
-        def needs(op):
-            kind, a = op[0], op[1:]
-            if kind == "ev_e":
-                return [("tr_e",) + a]
-            if kind == "q_e":
-                return [("ev_e",) + a] if len(a) >= 3 else [("ev_e",) + a + (tp,) for tp in range(2)]
-            if kind == "q_g":
-                return [("il_g",) + a]
-            if kind == "ev_kw":
-                return [("tr_kw",)]
-            if kind == "q_kw":
-                return [("ev_kw",)]
-            if kind == "q_x":
-                return [("il_x",) + a]
-            if kind == "mm_s1":
-                n, kv, t = a
-                first = (t,) if (kv, n, t // 2) == (0, 0, 0) and FINE else ()
-                return [("q_e", kv, n % 2, t // 2) + first, ("q_g", kv, n // 2)]
-            if kind == "ev_s1":
-                return [("mm_s1",) + a]
-            if kind == "tr_d":
-                n, t = a
-                return [("ev_s1", n, 0, t), ("ev_s1", n, 1, t)]
-            if kind == "ev_t":
-                n, t = a
-                return [("tr_d",) + a] + ([("q_f", n - 2, tp) for tp in range(2)] if n > 1 else [])
-            if kind == "q_f":
-                if len(a) == 1:
-                    return [("ev_t", a[0], t) for t in range(4)]
-                return [("ev_t", a[0], 2 * a[1] + t) for t in (a[2:] or range(2))]
-            if kind == "mm_dx":
-                return [("q_f", a[0], a[1]), ("q_kw",)]
-            if kind in ("mm_dt", "mm_d1"):
-                return [("q_f",) + a[:3], ("q_kw",)]
-            if kind in ("ev_dx", "ev_dt", "ev_d1"):
-                return [("mm" + kind[2:],) + a]
-            if kind in ("st_dx", "st_o1"):
-                return [("ev" + kind[2:],) + a]
-            if kind == "st_d1":
-                return [("ev_d1",) + a]
-            if kind == "q_tk":
-                return [("il_t", a[0], a[2], a[1]), ("mm_o1", a[0] - 3, 1)]
-            if kind == "il_t":
-                n, kv = a[:2]
-                old = [("q_t", n - 2, b) for b in range(2)] if n > 1 else []
-                return [("ev_s1", n, kv, t) for t in range(4)] + old
-            if kind == "q_t":
-                n = a[0]
-                old = [("mm_o1", n - 3, s) for s in range(2)] if n > 2 else []
-                return [("il_t", n, 0), ("il_t", n, 1)] + old
-            if kind == "mm_o1":
-                return [("q_t",) + a, ("q_x", a[0])]
-            if kind == "ev_o1":
-                return [("mm_o1", 3, 1)]
+        def needs(step):
+            call, at = step[0], step[1:]
+            if call is take_col:
+                old = [(quant_col, 2 * (at[0] // 2) - 4 + s) for s in both] if at[0] >= 4 else []
+                return [(turn_dkv,) + at] + old
+            if call in filled_by:
+                return [(filled_by[call],) + at]
+            if call is quant_e:
+                return [(take_e,) + at]
+            if call is quant_g:
+                return [(mix_g,) + at + (b,) for b in both]
+            if call is quant_kw:
+                return [(take_kw,)]
+            if call is quant_x:
+                return [(mix_x,) + at]
+            if call is pass_dkv:
+                n, kv = divmod(at[0], 2)
+                return [(quant_e, kv, n % 2, at[1] // 2), (quant_g, kv, n // 2)]
+            if call is turn_dkv:
+                n, t = divmod(2 * at[0] + at[1], 4)
+                return [(take_dkv, 2 * n + kv, t) for kv in both]
+            if call is quant_col:
+                return [(take_col,) + at + (s,) for s in both]
+            if call is pass_dx:
+                return [(quant_col, at[0]), (quant_kw,)]
+            if call is mix_tok:
+                old = [(quant_tok, at[0] // 2 - 2, b) for b in both] if at[0] >= 4 else []
+                return [(take_dkv,) + at + (t,) for t in range(4)] + old
+            if call is quant_tok:
+                old = [(pass_dw, at[0] - 3, b) for b in both] if at[0] >= 3 else []
+                return [(mix_tok, 2 * at[0] + kv) for kv in both] + old
+            if call is pass_dw:
+                return [(quant_tok,) + at, (quant_x, at[0])]
+            if call is take_dw:
+                return [(pass_dw, 3, 1)]
+            if call is store_dx:
+                return [(take_dx,) + at]
+            if call is store_dw:
+                return [(take_dw,) + at]
             return []
 
-        calls = {
-            "tr_e": tr_e, "ev_e": ev_e, "q_e": q_e, "il_g": il_g, "q_g": q_g, "tr_kw": tr_kw, "ev_kw": ev_kw,
-            "q_kw": q_kw, "il_x": il_x, "q_x": q_x, "mm_s1": mm_s1, "ev_s1": ev_s1, "tr_d": tr_d, "ev_t": ev_t,
-            "q_f": q_f, "mm_dx": mm_dx, "ev_dx": ev_dx, "il_t": il_t, "q_t": q_t, "mm_o1": mm_o1, "ev_o1": ev_o1,
-            "mm_dt": mm_dt, "ev_dt": ev_dt, "mm_d1": mm_d1, "ev_d1": ev_d1, "q_tk": q_tk,
-            "st_dx": st_dx, "st_o1": st_o1, "st_d1": st_d1,
-        }
-        emptied_by = {"tr_e": "ev_e", "tr_kw": "ev_kw", "mm_s1": "ev_s1", "tr_d": "ev_t", "mm_dx": "ev_dx", "mm_dt": "ev_dt", "mm_d1": "ev_d1"}
-
-        parts = {"q_e": 4, "il_g": 4, "q_g": 4, "q_t": 3, "q_f": 4, "il_t": 4, "il_x": 3}
-
-        def write_in_order(queues):
-            fills = [op for op in queues["T"] if op[0] in emptied_by]
+        def write_in_order(orders):
+            fills = [step for step in orders["tensor"] if step[0] in emptied_by]
             written = set()
-            heads = {eng: 0 for eng in queues}
-            for sweep in range(sum(len(q) for q in queues.values())):
-                for eng in queues:
-                    if heads[eng] == len(queues[eng]):
+            heads = {eng: 0 for eng in orders}
+            for sweep in range(sum(len(order) for order in orders.values())):
+                for eng in orders:
+                    if heads[eng] == len(orders[eng]):
                         continue
-                    op = queues[eng][heads[eng]]
-                    wanted = needs(op)
-                    if op in fills and fills.index(op) >= ROTATING_BANKS:
-                        old = fills[fills.index(op) - ROTATING_BANKS]
-                        wanted = wanted + [(emptied_by[old[0]],) + old[1:]]
-                    if all(w in written for w in wanted):
-                        if op[0][:2] in ("ev", "il"):
-                            calls[op[0]](eng, *op[1:])
-                        else:
-                            calls[op[0]](*op[1:])
-                        written.add(op)
-                        if op[0] == "ev_dt":
-                            written.add(("ev_d1",) + op[1:] + (0,))
-                            written.add(("ev_d1",) + op[1:] + (1,))
-                        if op[0] == "q_tk" and op[:-1] + (1 - op[-1],) in written:
-                            written.add(("q_t",) + op[1:3])
-                        if len(op) < parts.get(op[0], 0):
-                            written.add(op + (0,))
-                            written.add(op + (1,))
-                        elif len(op) == 5 and op[0] == "q_e":
-                            if op[-1] == 1:
-                                written.add(op[:-1])
-                        elif op[0] in parts and op[:-1] + (1 - op[-1],) in written:
-                            written.add(op[:-1])
+                    step = orders[eng][heads[eng]]
+                    wanted = [need for part in halves(step) for need in needs(part)]
+                    if step in fills and fills.index(step) >= ROTATING_BANKS:
+                        old = fills[fills.index(step) - ROTATING_BANKS]
+                        wanted.append((emptied_by[old[0]],) + old[1:])
+                    if all(need in written for need in wanted):
+                        reads_psum = step[0] in filled_by or step[0] is take_dw
+                        step[0](*(((eng,) if reads_psum else ()) + step[1:]))
+                        for part in halves(step):
+                            written.add(part)
                         heads[eng] = heads[eng] + 1
-            assert all(heads[eng] == len(queues[eng]) for eng in queues)
+            assert all(heads[eng] == len(orders[eng]) for eng in orders)
+
+        def each(call, at, last):
+            return [(call,) + at + (s,) for s in last]
+
+        back = (1, 0)
+        low, high = (0, 1), (2, 3)
+        low_back, high_back = (1, 0), (3, 2)
+
+        tensor = each(turn_e, (0, 0), both) + [(turn_e, 0, 1, 0)] + each(pass_dkv, (0,), low)
+        tensor += [(turn_e, 0, 1, 1)] + each(pass_dkv, (0,), high)
+        tensor += each(turn_e, (1, 0), both) + each(pass_dkv, (2,), low)
+        tensor += each(turn_e, (1, 1), both) + each(pass_dkv, (2,), high)
+        tensor += each(pass_dkv, (1,), low) + [(turn_kw,)] + each(pass_dkv, (1,), high) + each(turn_dkv, (0,), both)
+        tensor += each(pass_dkv, (3,), low) + each(turn_dkv, (1,), both)
+        tensor += each(pass_dkv, (3,), high) + each(turn_dkv, (2,), both)
+        scalar = each(take_e, (0, 0), both) + [(take_e, 0, 1, 0)] + each(take_dkv, (0,), low)
+        scalar += [(take_e, 0, 1, 1)] + each(take_dkv, (0,), high)
+        scalar += [(take_e, 1, 0, 0)] + each(take_dkv, (2,), low_back)
+        scalar += each(take_e, (1, 1), back) + each(take_dkv, (2,), high_back)
+        scalar += each(take_dkv, (1,), low_back) + [(take_kw,)] + each(take_dkv, (1,), high_back)
+        scalar += each(take_col, (0,), back) + each(take_dkv, (3,), low_back) + each(take_col, (1,), back)
+        scalar += each(take_dkv, (3,), high_back) + each(take_col, (2,), back)
+
+        vector_takes = [(take_dx, 0, 0), (take_dx, 5, 0), (take_dx, 7, 1)]
+        for j in range(4, 8):
+            tensor += each(pass_dkv, (j,), low) + each(pass_dx, (j - DX_LAG,), both) + each(pass_dkv, (j,), high)
+            if j > 4:
+                tensor += each(pass_dw, (j - 5,), both)
+            tensor += each(turn_dkv, (j - 1,), both)
+            scalar += each(take_dkv, (j,), low_back) + each(take_dx, (j - DX_LAG,), back)
+            scalar += each(take_dkv, (j,), high_back) + each(take_col, (j - 1,), back)
+
+        tensor += each(pass_dx, (4,), both) + each(pass_dx, (5,), both) + each(turn_dkv, (7,), both)
+        tensor += each(pass_dx, (6,), both) + each(pass_dw, (3,), both) + each(pass_dx, (7,), both)
+        scalar += each(take_dx, (4,), back) + each(take_dx, (5,), back) + each(take_col, (7,), back)
+        scalar += each(take_dx, (6,), both) + [(take_dw, 0)] + each(take_dx, (7,), both)
+        scalar = [step for step in scalar if step not in vector_takes]
+
+        vector = each(mix_g, (0, 0), both) + [(quant_e, 0, 0, 0), (quant_g, 0, 0), (quant_e, 0, 0, 1)]
+        vector += [(mix_g, 1, 0, 0), (quant_e, 0, 1, 0), (mix_g, 1, 0, 1), (quant_g, 1, 0), (quant_e, 0, 1, 1)]
+        vector += [(take_e, 1, 0, 1), (mix_tok, 0), (quant_e, 1, 0), (mix_g, 0, 1), (quant_e, 1, 1), (mix_g, 1, 1)]
+        vector += [(quant_g, 0, 1), (mix_tok, 2), (quant_g, 1, 1), (quant_kw,)]
+        vector += [(mix_x, 0), (quant_col, 0), (quant_x, 0), (mix_tok, 1), (quant_col, 1), (quant_tok, 0)]
+        vector += [vector_takes[0], (mix_x, 1), (quant_col, 2), (mix_tok, 3), (quant_x, 1)]
+        vector += [(mix_x, 2), (quant_tok, 1), (quant_col, 3), (quant_x, 2)]
+        vector += [(mix_tok, 4), (mix_tok, 5), (quant_col, 4), (quant_tok, 2)]
+        vector += [(mix_x, 3), (quant_col, 5), (mix_tok, 6), (quant_x, 3)]
+        vector += [(mix_tok, 7), (quant_col, 6), vector_takes[1]] + each(quant_tok, (3,), both)
+        vector += [(quant_col, 7), (take_dw, 1), vector_takes[2]]
+
+        stores = []
+        for f in range(6):
+            stores += each(store_dx, (f,), back)
+        stores += each(store_dx, (6,), both) + each(store_dw, (), both) + each(store_dx, (7,), both)
 
         with tc.manual_schedule():
             make_identity(nc, ident[:])
@@ -458,48 +426,4 @@ def tile_efficientspatialwindowattention_pa_v_kernel(
             for n in range(4):
                 for b in range(2):
                     load_x(n, b)
-
-            def s1(kind, n, kv, ts):
-                return [(kind, n, kv, t) for t in ts]
-
-            def half(kind, f):
-                return [(kind, f // 2, f % 2)]
-
-            def tpair(kind, f, ts):
-                return [(kind, f // 2, 2 * (f % 2) + t) for t in ts]
-
-            def dxs(kind, f, bs):
-                return [(kind, f // 2, f % 2, b) for b in bs]
-
-            def ee(kind, kv, h, tps=(0, 1)):
-                return [(kind, kv, h, tp) for tp in tps]
-
-
-            te = ee("tr_e", 0, 0) + ee("tr_e", 0, 1, (0,)) + s1("mm_s1", 0, 0, (0, 1)) + ee("tr_e", 0, 1, (1,)) + s1("mm_s1", 0, 0, (2, 3))
-            te += ee("tr_e", 1, 0) + s1("mm_s1", 1, 0, (0, 1)) + ee("tr_e", 1, 1) + s1("mm_s1", 1, 0, (2, 3))
-            te += s1("mm_s1", 0, 1, (0, 1)) + [("tr_kw",)] + s1("mm_s1", 0, 1, (2, 3)) + tpair("tr_d", 0, (0, 1))
-            te += s1("mm_s1", 1, 1, (0, 1)) + tpair("tr_d", 1, (0, 1)) + s1("mm_s1", 1, 1, (2, 3)) + tpair("tr_d", 2, (0, 1))
-            sc = ee("ev_e", 0, 0) + ee("ev_e", 0, 1, (0,)) + s1("ev_s1", 0, 0, (0, 1)) + ee("ev_e", 0, 1, (1,)) + s1("ev_s1", 0, 0, (2, 3))
-            sc += ee("ev_e", 1, 0, (0,)) + s1("ev_s1", 1, 0, (1, 0)) + ee("ev_e", 1, 1, (1, 0)) + s1("ev_s1", 1, 0, (3, 2))
-            sc += s1("ev_s1", 0, 1, (1, 0)) + [("ev_kw",)] + s1("ev_s1", 0, 1, (3, 2)) + tpair("ev_t", 0, (1, 0))
-            sc += s1("ev_s1", 1, 1, (1, 0)) + tpair("ev_t", 1, (1, 0)) + s1("ev_s1", 1, 1, (3, 2)) + tpair("ev_t", 2, (1, 0))
-            ve = [("il_g", 0, 0, 0), ("il_g", 0, 0, 1), ("q_e", 0, 0, 0), ("q_g", 0, 0), ("q_e", 0, 0, 1), ("il_g", 1, 0, 0), ("q_e", 0, 1, 0)]
-            ve += [("il_g", 1, 0, 1), ("q_g", 1, 0), ("q_e", 0, 1, 1), ("ev_e", 1, 0, 1), ("il_t", 0, 0), ("q_e", 1, 0), ("il_g", 0, 1)]
-            ve += [("q_e", 1, 1), ("il_g", 1, 1), ("q_g", 0, 1), ("il_t", 1, 0), ("q_g", 1, 1), ("q_kw",)]
-            ve += [("il_x", 0), ("q_f", 0, 0), ("q_x", 0), ("il_t", 0, 1), ("q_f", 0, 1), ("il_x", 1), ("q_t", 0)]
-            ve += [("q_f", 1, 0), ("il_t", 1, 1), ("q_x", 1)]
-            for j in range(4, 8):
-                n, kv = divmod(j, 2)
-                te += s1("mm_s1", n, kv, (0, 1)) + dxs("mm_dx", j - 4, (0, 1)) + s1("mm_s1", n, kv, (2, 3))
-                te += (half("mm_o1", 2 * j - 10) + half("mm_o1", 2 * j - 9) if 4 < j else []) + tpair("tr_d", j - 1, (0, 1))
-                sc += s1("ev_s1", n, kv, (1, 0)) + dxs("ev_dx", j - 4, (1, 0)) + s1("ev_s1", n, kv, (3, 2)) + tpair("ev_t", j - 1, (1, 0))
-            ve += [("il_x", 2), ("q_t", 1), ("q_f", 1, 1), ("q_x", 2), ("il_t", 2, 0), ("il_t", 2, 1), ("q_f", 2, 0)]
-            ve += [("q_t", 2), ("il_x", 3), ("q_f", 2, 1), ("il_t", 3, 0), ("q_x", 3)]
-            te += dxs("mm_dx", 4, (0, 1)) + dxs("mm_dx", 5, (0, 1)) + tpair("tr_d", 7, (0, 1)) + dxs("mm_dx", 6, (0, 1)) + half("mm_o1", 6) + half("mm_o1", 7) + dxs("mm_dx", 7, (0, 1))
-            sc += dxs("ev_dx", 4, (1, 0)) + dxs("ev_dx", 5, (1,)) + tpair("ev_t", 7, (1, 0)) + dxs("ev_dx", 6, (0,1)) + [("ev_o1", 0)] + dxs("ev_dx", 7, (0,))
-            ve += [("il_t", 3, 1), ("q_f", 3, 0), ("ev_dx", 2, 1, 0), ("q_t", 3, 0), ("q_t", 3, 1), ("q_f", 3, 1)] + [("ev_o1", 1)] + dxs("ev_dx", 7, (1,))
-            st = []
-            for f in range(5):
-                st += dxs("st_dx", f, (1, 0))
-            st += dxs("st_dx", 5, (1, 0)) + dxs("st_dx", 6, (0, 1)) + [("st_o1", 0), ("st_o1", 1)] + dxs("st_dx", 7, (0, 1))
-            write_in_order({"T": te, "S": sc, "V": ve, "Q": st})
+            write_in_order({"tensor": tensor, "scalar": scalar, "vector": vector, "sync": stores})

from contextlib import ExitStack

import concourse.mybir as mybir
from concourse.masks import make_identity

F32 = mybir.dt.float32
BF16 = mybir.dt.bfloat16
U32 = mybir.dt.uint32
U8 = mybir.dt.uint8
E4M3 = mybir.dt.float8_e4m3fn_x4
E5M2 = mybir.dt.float8_e5m2_x4

FLOPS = 2 * 2 * 4 * 1024 * 512 * 256 + 2 * 2 * 4096 * 512 * 256

ROTATING_BANKS = 6
DX_LAG = 4


def tile_efficientspatialwindowattention_pa_v_kernel(
    tc, x, kv_w, kv_b, e_k, e_v, grad_0, grad_1, out_0, out_1
):
    nc = tc.nc
    es = (e_k, e_v)
    grads = (grad_0, grad_1)
    x_view = x.rearrange("o (a h r b q t) c -> a b h o r q (t c)", a=2, h=2, r=16, b=2, q=8, t=4)
    dx_view = out_0.rearrange("o (n g p t) c -> o n g p (t c)", n=4, g=2, t=4)[0]

    with ExitStack() as ctx:
        keep = ctx.enter_context(tc.tile_pool(name="keep", bufs=1))
        rot = ctx.enter_context(tc.tile_pool(name="rot", bufs=2))
        psum = ctx.enter_context(tc.psum_pool(name="psum", bufs=1))

        def kept(width, dtype, name, on=None):
            return keep.tile([128, width], dtype, name=name, tag=on or name, align_bytes=64)

        ident = kept(128, F32, "ident")
        e_raw, e_in, e_codes, e_scales = {}, {}, {}, {}
        g_raw, g_in, g_codes, g_scales = {}, {}, {}, {}
        for kv in range(2):
            for h in range(2):
                for tp in range(2):
                    e_raw[kv, h, tp] = kept(1024, BF16, "e_raw_%d%d%d" % (kv, h, tp))
                e_codes[kv, h] = kept(512, U32, "e_codes_%d%d" % (kv, h))
                e_scales[kv, h] = kept(512, U8, "e_scales_%d%d" % (kv, h))
            for a in range(2):
                g_raw[kv, a] = kept(2048, BF16, "g_raw_%d%d" % (kv, a))
                g_codes[kv, a] = kept(512, U32, "g_codes_%d%d" % (kv, a))
                g_scales[kv, a] = kept(512, U8, "g_scales_%d%d" % (kv, a))
        x_raw, x_in, x_codes, x_scales = {}, {}, {}, {}
        for n in range(4):
            x_raw[n] = kept(2048, BF16, "x_raw_%d" % n)
            x_codes[n] = kept(512, U32, "x_codes_%d" % n)
            x_scales[n] = kept(512, U8, "x_scales_%d" % n)
        kw_raw = kept(1024, BF16, "kw_raw")
        kw_in = kept(1024, BF16, "kw_in")
        kw_codes = kept(768, U32, "kw_codes")
        kw_scales = kept(768, U8, "kw_scales")

        dkv, tok_in, tok_codes, tok_scales, col_in, col_codes, col_scales = {}, {}, {}, {}, {}, {}, {}
        banks, dx, dw_banks, dw = {}, {}, {}, {}
        spent = ["e_in_%d%d" % key for key in e_codes] + ["g_in_%d%d" % key for key in g_codes]

        def next_bank(key):
            tag = "bank_%d" % (len(banks) % ROTATING_BANKS)
            banks[key] = psum.tile([128, 512], F32, name="bank", tag=tag)
            return banks[key]

        def copy(eng, out, in_):
            if eng == "vector":
                nc.vector.tensor_copy(out=out, in_=in_)
            else:
                nc.scalar.copy(out=out, in_=in_)

        def quantize(codes, scales, values, fmt, lo, hi):
            nc.vector.quantize_mx(
                out=codes[:, lo:hi].bitcast(fmt), scales=scales[:, lo:hi], in_=values[:, 4 * lo : 4 * hi]
            )

        def span(part, width):
            return (0, width) if part is None else (part * width // 2, (part + 1) * width // 2)


        def load_e(kv, h, tp):
            src = es[kv].rearrange("(h p tp t) j -> h tp p (t j)", h=2, tp=2, t=2)
            nc.sync.dma_start(out=e_raw[kv, h, tp][:], in_=src[h, tp])

        def load_g(kv, a, b=None):
            src = grads[kv].rearrange("(a b) h (p j) d -> a p (b h) (j d)", b=2, j=4)[a]
            dst = g_raw[kv, a][:].rearrange("p (s f) -> p s f", s=8)
            lo, hi = span(b, 8)
            nc.sync.dma_start(out=dst[:, lo:hi, :], in_=src[:, lo:hi, :])

        def load_x(n, b):
            nc.sync.dma_start(out=x_raw[n][:, 1024 * b : 1024 * b + 1024], in_=x_view[n // 2, b, n % 2, 0])

        def load_kw():
            nc.sync.dma_start(
                out=kw_raw[:].rearrange("p (m k) -> p m k", m=2), in_=kv_w.rearrange("(m p) k -> p m k", m=2)
            )

        def store_dx(f, g):
            n, tp = divmod(f, 2)
            nc.sync.dma_start(
                out=dx_view[n, g][:, 512 * tp : 512 * tp + 512], in_=dx[f][:, 512 * g : 512 * g + 512]
            )

        def store_dw(m):
            nc.sync.dma_start(out=out_1[128 * m : 128 * m + 128, :], in_=dw[m][:])


        def transpose_rows(raw, key):
            bank = next_bank(key)
            for row in range(2):
                words = raw[:, 512 * row : 512 * row + 512].bitcast(F32)
                for u in range(2):
                    c0 = (2 * row + u) * 128
                    nc.tensor.transpose(bank[:, c0 : c0 + 128], words[:, u::2], ident[:])

        def join_words(eng, dst, key):
            copy(
                eng,
                dst.bitcast(F32).rearrange("p (row c u) -> p row c u", row=2, u=2),
                banks[key][:].rearrange("p (row u c) -> p row c u", row=2, u=2),
            )

        def turn_e(kv, h, tp):
            transpose_rows(e_raw[kv, h, tp], ("e", kv, h, tp))

        def take_e(eng, kv, h, tp):
            if (kv, h) not in e_in:
                e_in[kv, h] = kept(2048, BF16, "e_in_%d%d" % (kv, h))
            join_words(eng, e_in[kv, h][:, 1024 * tp : 1024 * tp + 1024], ("e", kv, h, tp))

        def quant_e(kv, h, tp=None):
            quantize(e_codes[kv, h], e_scales[kv, h], e_in[kv, h], E4M3, *span(tp, 512))

        def turn_kw():
            transpose_rows(kw_raw, "kw")

        def take_kw(eng):
            join_words(eng, kw_in[:], "kw")

        def quant_kw():
            nc.vector.quantize_mx(
                out=kw_codes[:, 256:512].bitcast(E4M3), scales=kw_scales[:, 256:512], in_=kw_in[:]
            )


        def mix_g(kv, a, b=None):
            if (kv, a) not in g_in:
                g_in[kv, a] = kept(2048, BF16, "g_in_%d%d" % (kv, a))
            lo, hi = span(b, 2048)
            nc.vector.tensor_copy(
                out=g_in[kv, a][:, lo:hi].rearrange("p (h d i j) -> p h d j i", d=16, i=4, j=4),
                in_=g_raw[kv, a][:, lo:hi].rearrange("p (h j d i) -> p h d j i", d=16, j=4, i=4),
            )

        def quant_g(kv, a):
            quantize(g_codes[kv, a], g_scales[kv, a], g_in[kv, a], E5M2, 0, 512)

        def mix_x(n):
            x_in[n] = kept(2048, BF16, "x_in_%d" % n)
            nc.vector.tensor_copy(
                out=x_in[n][:].rearrange("p (b c i t) -> p b c t i", b=2, i=4, t=4),
                in_=x_raw[n][:].rearrange("p (b t c i) -> p b c t i", b=2, i=4, t=4),
            )

        def quant_x(n):
            quantize(x_codes[n], x_scales[n], x_in[n], E4M3, 0, 512)


        def pass_dkv(j, t):
            n, kv = divmod(j, 2)
            cols = slice(128 * t, 128 * t + 128)
            nc.tensor.matmul_mx(
                out=next_bank(("dkv", j, t))[:],
                lhsT=e_codes[kv, n % 2][:, cols].bitcast(E4M3),
                lhsT_scale=e_scales[kv, n % 2][:, cols],
                rhs=g_codes[kv, n // 2][:].bitcast(E5M2),
                rhs_scale=g_scales[kv, n // 2][:],
                start=True,
                stop=True,
            )

        def take_dkv(eng, j, t):
            n, kv = divmod(j, 2)
            if n not in dkv:
                dkv[n] = rot.tile([128, 4096], BF16, name="dkv", bufs=4, align_bytes=64)
            dst = dkv[n][:].rearrange("p (t b u k i e) -> p t k b u i e", t=4, b=2, u=2, k=2, e=2)[:, t, kv]
            copy(eng, dst, banks["dkv", j, t][:].rearrange("p (b i u e) -> p b u i e", b=2, u=2, e=2))


        def turn_dkv(f, s):
            n, t = divmod(2 * f + s, 4)
            bank = next_bank(("col", f, s))
            words = dkv[n][:, 1024 * t : 1024 * t + 1024].bitcast(F32)
            for bu in range(4):
                cols = slice(128 * bu, 128 * bu + 128)
                nc.tensor.transpose(bank[:, cols], words[:, cols], ident[:])

        def take_col(eng, f, s):
            n, t = divmod(2 * f + s, 4)
            if n not in col_in:
                col_in[n] = rot.tile([128, 4096], BF16, name="col_in", align_bytes=64)
            dst = col_in[n][:, 1024 * t : 1024 * t + 1024].bitcast(F32)
            copy(
                eng,
                dst.rearrange("p (r b q u) -> p r b q u", b=2, q=8, u=2),
                banks["col", f, s][:].rearrange("p (b u r q) -> p r b q u", b=2, q=8, u=2),
            )

        def quant_col(f):
            n, tp = divmod(f, 2)
            if n not in col_codes:
                col_codes[n] = kept(1024, U32, "col_codes_%d" % n)
                col_scales[n] = kept(1024, U8, "col_scales_%d" % n)
            quantize(col_codes[n], col_scales[n], col_in[n], E5M2, *span(tp, 1024))

        def pass_dx(f, g):
            n, tp = divmod(f, 2)
            bank = next_bank(("dx", f, g))
            for s in range(2):
                c0 = 256 * (2 * tp + s) + 128 * g
                win = slice(256, 768) if s == 0 else slice(0, 512)
                nc.tensor.matmul_mx(
                    out=bank[:],
                    lhsT=col_codes[n][:, c0 : c0 + 128].bitcast(E5M2),
                    lhsT_scale=col_scales[n][:, c0 : c0 + 128],
                    rhs=kw_codes[:, win].bitcast(E4M3),
                    rhs_scale=kw_scales[:, win],
                    start=(s == 0),
                    stop=(s == 1),
                )

        def take_dx(eng, f, g):
            if f not in dx:
                dx[f] = kept(1024, F32, "dx", spent[f])
            copy(eng, dx[f][:, 512 * g : 512 * g + 512], banks["dx", f, g][:])


        def mix_tok(j):
            n, kv = divmod(j, 2)
            if n not in tok_in:
                tok_in[n] = rot.tile([128, 4096], BF16, name="tok_in", align_bytes=64)
            nc.vector.tensor_copy(
                out=tok_in[n][:].rearrange("p (bu k c i t) -> p k bu c t i", bu=4, k=2, i=4, t=4)[:, kv],
                in_=dkv[n][:].rearrange("p (t bu k c i) -> p k bu c t i", t=4, bu=4, k=2, i=4)[:, kv],
            )

        def quant_tok(n, b=None):
            if n not in tok_codes:
                tok_codes[n] = rot.tile([128, 1024], U32, name="tok_codes", bufs=3, align_bytes=64)
                tok_scales[n] = rot.tile([128, 1024], U8, name="tok_scales", bufs=3, align_bytes=64)
            quantize(tok_codes[n], tok_scales[n], tok_in[n], E5M2, *span(b, 1024))

        def pass_dw(n, b):
            for m in range(2):
                if m not in dw_banks:
                    dw_banks[m] = psum.tile([128, 512], F32, name="held", tag="held_%d" % m)
                cols = slice(256 * b + 128 * m, 256 * b + 128 * m + 128)
                win = slice(512 * b, 512 * b + 512)
                nc.tensor.matmul_mx(
                    out=dw_banks[m][:],
                    lhsT=x_codes[n][:, cols].bitcast(E4M3),
                    lhsT_scale=x_scales[n][:, cols],
                    rhs=tok_codes[n][:, win].bitcast(E5M2),
                    rhs_scale=tok_scales[n][:, win],
                    start=(n == 0 and b == 0),
                    stop=(n == 3 and b == 1),
                )

        def take_dw(eng, m):
            dw[m] = kept(512, F32, "dw_%d" % m)
            copy(
                eng,
                dw[m][:].rearrange("p (i u e) -> p i u e", u=2, e=2),
                dw_banks[m][:].rearrange("p (u i e) -> p i u e", u=2, e=2),
            )


        both = (0, 1)
        indices = {quant_e: 3, mix_g: 3, quant_tok: 2}
        emptied_by = {turn_e: take_e, turn_kw: take_kw, pass_dkv: take_dkv, turn_dkv: take_col, pass_dx: take_dx}
        filled_by = {take: fill for fill, take in emptied_by.items()}

        def halves(step):
            whole = len(step) - 1 < indices.get(step[0], 0)
            return [step + (s,) for s in both] if whole else [step]

        def needs(step):
            call, at = step[0], step[1:]
            if call is take_col:
                old = [(quant_col, 2 * (at[0] // 2) - 4 + s) for s in both] if at[0] >= 4 else []
                return [(turn_dkv,) + at] + old
            if call in filled_by:
                return [(filled_by[call],) + at]
            if call is quant_e:
                return [(take_e,) + at]
            if call is quant_g:
                return [(mix_g,) + at + (b,) for b in both]
            if call is quant_kw:
                return [(take_kw,)]
            if call is quant_x:
                return [(mix_x,) + at]
            if call is pass_dkv:
                n, kv = divmod(at[0], 2)
                return [(quant_e, kv, n % 2, at[1] // 2), (quant_g, kv, n // 2)]
            if call is turn_dkv:
                n, t = divmod(2 * at[0] + at[1], 4)
                return [(take_dkv, 2 * n + kv, t) for kv in both]
            if call is quant_col:
                return [(take_col,) + at + (s,) for s in both]
            if call is pass_dx:
                return [(quant_col, at[0]), (quant_kw,)]
            if call is mix_tok:
                old = [(quant_tok, at[0] // 2 - 2, b) for b in both] if at[0] >= 4 else []
                return [(take_dkv,) + at + (t,) for t in range(4)] + old
            if call is quant_tok:
                old = [(pass_dw, at[0] - 3, b) for b in both] if at[0] >= 3 else []
                return [(mix_tok, 2 * at[0] + kv) for kv in both] + old
            if call is pass_dw:
                return [(quant_tok,) + at, (quant_x, at[0])]
            if call is take_dw:
                return [(pass_dw, 3, 1)]
            if call is store_dx:
                return [(take_dx,) + at]
            if call is store_dw:
                return [(take_dw,) + at]
            return []

        def write_in_order(orders):
            fills = [step for step in orders["tensor"] if step[0] in emptied_by]
            written = set()
            heads = {eng: 0 for eng in orders}
            for sweep in range(sum(len(order) for order in orders.values())):
                for eng in orders:
                    if heads[eng] == len(orders[eng]):
                        continue
                    step = orders[eng][heads[eng]]
                    wanted = [need for part in halves(step) for need in needs(part)]
                    if step in fills and fills.index(step) >= ROTATING_BANKS:
                        old = fills[fills.index(step) - ROTATING_BANKS]
                        wanted.append((emptied_by[old[0]],) + old[1:])
                    if all(need in written for need in wanted):
                        reads_psum = step[0] in filled_by or step[0] is take_dw
                        step[0](*(((eng,) if reads_psum else ()) + step[1:]))
                        for part in halves(step):
                            written.add(part)
                        heads[eng] = heads[eng] + 1
            assert all(heads[eng] == len(orders[eng]) for eng in orders)

        def each(call, at, last):
            return [(call,) + at + (s,) for s in last]

        back = (1, 0)
        low, high = (0, 1), (2, 3)
        low_back, high_back = (1, 0), (3, 2)

        tensor = each(turn_e, (0, 0), both) + [(turn_e, 0, 1, 0)] + each(pass_dkv, (0,), low)
        tensor += [(turn_e, 0, 1, 1)] + each(pass_dkv, (0,), high)
        tensor += each(turn_e, (1, 0), both) + each(pass_dkv, (2,), low)
        tensor += each(turn_e, (1, 1), both) + each(pass_dkv, (2,), high)
        tensor += each(pass_dkv, (1,), low) + [(turn_kw,)] + each(pass_dkv, (1,), high) + each(turn_dkv, (0,), both)
        tensor += each(pass_dkv, (3,), low) + each(turn_dkv, (1,), both)
        tensor += each(pass_dkv, (3,), high) + each(turn_dkv, (2,), both)
        scalar = each(take_e, (0, 0), both) + [(take_e, 0, 1, 0)] + each(take_dkv, (0,), low)
        scalar += [(take_e, 0, 1, 1)] + each(take_dkv, (0,), high)
        scalar += [(take_e, 1, 0, 0)] + each(take_dkv, (2,), low_back)
        scalar += each(take_e, (1, 1), back) + each(take_dkv, (2,), high_back)
        scalar += each(take_dkv, (1,), low_back) + [(take_kw,)] + each(take_dkv, (1,), high_back)
        scalar += each(take_col, (0,), back) + each(take_dkv, (3,), low_back) + each(take_col, (1,), back)
        scalar += each(take_dkv, (3,), high_back) + each(take_col, (2,), back)

        vector_takes = [(take_dx, 0, 0), (take_dx, 5, 0), (take_dx, 7, 1)]
        for j in range(4, 8):
            tensor += each(pass_dkv, (j,), low) + each(pass_dx, (j - DX_LAG,), both) + each(pass_dkv, (j,), high)
            if j > 4:
                tensor += each(pass_dw, (j - 5,), both)
            tensor += each(turn_dkv, (j - 1,), both)
            scalar += each(take_dkv, (j,), low_back) + each(take_dx, (j - DX_LAG,), back)
            scalar += each(take_dkv, (j,), high_back) + each(take_col, (j - 1,), back)

        tensor += each(pass_dx, (4,), both) + each(pass_dx, (5,), both) + each(turn_dkv, (7,), both)
        tensor += each(pass_dx, (6,), both) + each(pass_dw, (3,), both) + each(pass_dx, (7,), both)
        scalar += each(take_dx, (4,), back) + each(take_dx, (5,), back) + each(take_col, (7,), back)
        scalar += each(take_dx, (6,), both) + [(take_dw, 0)] + each(take_dx, (7,), both)
        scalar = [step for step in scalar if step not in vector_takes]

        vector = each(mix_g, (0, 0), both) + [(quant_e, 0, 0, 0), (quant_g, 0, 0), (quant_e, 0, 0, 1)]
        vector += [(mix_g, 1, 0, 0), (quant_e, 0, 1, 0), (mix_g, 1, 0, 1), (quant_g, 1, 0), (quant_e, 0, 1, 1)]
        vector += [(take_e, 1, 0, 1), (mix_tok, 0), (quant_e, 1, 0), (mix_g, 0, 1), (quant_e, 1, 1), (mix_g, 1, 1)]
        vector += [(quant_g, 0, 1), (mix_tok, 2), (quant_g, 1, 1), (quant_kw,)]
        vector += [(mix_x, 0), (quant_col, 0), (quant_x, 0), (mix_tok, 1), (quant_col, 1), (quant_tok, 0)]
        vector += [vector_takes[0], (mix_x, 1), (quant_col, 2), (mix_tok, 3), (quant_x, 1)]
        vector += [(mix_x, 2), (quant_tok, 1), (quant_col, 3), (quant_x, 2)]
        vector += [(mix_tok, 4), (mix_tok, 5), (quant_col, 4), (quant_tok, 2)]
        vector += [(mix_x, 3), (quant_col, 5), (mix_tok, 6), (quant_x, 3)]
        vector += [(mix_tok, 7), (quant_col, 6), vector_takes[1]] + each(quant_tok, (3,), both)
        vector += [(quant_col, 7), (take_dw, 1), vector_takes[2]]

        stores = []
        for f in range(6):
            stores += each(store_dx, (f,), back)
        stores += each(store_dx, (6,), both) + each(store_dw, (), both) + each(store_dx, (7,), both)

        with tc.manual_schedule():
            make_identity(nc, ident[:])
            nc.gpsimd.memset(kw_codes[:, 0:256], 0)
            nc.gpsimd.memset(kw_codes[:, 512:768], 0)
            nc.gpsimd.memset(kw_scales[:].bitcast(U32)[:, 0:64], 0)
            nc.gpsimd.memset(kw_scales[:].bitcast(U32)[:, 128:192], 0)
            load_e(0, 0, 0)
            load_g(0, 0, 0)
            load_g(0, 0, 1)
            load_e(0, 0, 1)
            load_e(0, 1, 0)
            load_e(0, 1, 1)
            load_g(1, 0, 0)
            load_g(1, 0, 1)
            for h in range(2):
                for tp in range(2):
                    load_e(1, h, tp)
            load_kw()
            for kv in range(2):
                load_g(kv, 1)
            for n in range(4):
                for b in range(2):
                    load_x(n, b)
            write_in_order({"tensor": tensor, "scalar": scalar, "vector": vector, "sync": stores})
